import numpy as np
import ml_dtypes


def mxq(x, axis, fmt="e4m3"):
    dtype, down = {"e4m3": (ml_dtypes.float8_e4m3fn, 7), "e5m2": (ml_dtypes.float8_e5m2, 14)}[fmt]
    v = np.moveaxis(np.asarray(x, np.float32).astype(ml_dtypes.bfloat16).astype(np.float64), axis, -1)
    blocks = v.reshape(v.shape[:-1] + (-1, 32))
    amax = np.abs(blocks).max(-1, keepdims=True)
    byte = np.maximum(np.where(amax > 0, np.frexp(amax)[1] - 1 + 127, 0) - down, 1)
    scale = np.exp2(byte - 127.0)
    codes = (blocks / scale).astype(np.float32).astype(dtype).astype(np.float64)
    return np.moveaxis((codes * scale).reshape(v.shape), -1, axis)


WIDE = False


def mx_kscale(k):
    if not WIDE:
        return np.ones(k)
    levels = np.array([10, -10, 5, -5, 0])
    a = np.random.permutation(np.resize(levels, k // 512 * 4)).reshape(k // 512, 4)
    idx = np.arange(k)
    return np.exp2(a[idx // 512, idx % 128 // 32])


BF16 = ml_dtypes.bfloat16


def bf(x):
    return np.asarray(x, np.float32).astype(BF16)


def f64(x):
    return np.asarray(x).astype(np.float64)


B, S, HID, NH = 4, 128, 2048, 16
LN_EPS = 1e-5


def sigmoid(v):
    return 1.0 / (1.0 + np.exp(-v))


def setup_inputs():
    s = mx_kscale(HID)
    w = 1.0 / np.sqrt(HID)
    return {"hidden_states": bf(np.random.standard_normal((B, S, HID))),
            "attn_ctx": bf(np.random.standard_normal((B, S, HID)) * 0.3 * s),
            "Wo": bf(np.random.standard_normal((HID, HID)) * 3.0 * w / s[:, None]),
            "bo": bf(np.random.standard_normal(HID) * 0.3 + 0.3),
            "Wg": bf(np.random.standard_normal((HID, HID)) * w),
            "bg": bf(np.random.standard_normal(HID) * 0.5),
            "ln_gamma": bf(1.0 + 0.1 * np.random.standard_normal(HID)),
            "ln_beta": bf(0.1 * np.random.standard_normal(HID))}


def reference(hidden_states, attn_ctx, Wo, bo, Wg, bg, ln_gamma, ln_beta):
    h = f64(hidden_states)
    attn = (mxq(f64(attn_ctx), 2, "e4m3") @ mxq(f64(Wo), 0, "e4m3")) + f64(bo)
    gate = sigmoid((mxq(h, 2, "e4m3") @ mxq(f64(Wg), 0, "e4m3")) + f64(bg))
    y = h + gate * attn
    mu = y.mean(-1, keepdims=True)
    var = np.square(y - mu).mean(-1, keepdims=True)
    return (y - mu) / np.sqrt(var + LN_EPS) * f64(ln_gamma) + f64(ln_beta)

@@ -1,0 +1,214 @@
+from contextlib import ExitStack
+
+import concourse.mybir as mybir
+from concourse.masks import make_identity
+
+F32 = mybir.dt.float32
+BF16 = mybir.dt.bfloat16
+U32 = mybir.dt.uint32
+U8 = mybir.dt.uint8
+FP8X4 = mybir.dt.float8_e4m3fn_x4
+ALU = mybir.AluOpType
+ACT = mybir.ActivationFunctionType
+
+P = 128
+PACK = 4
+K_PASS = P * PACK
+HID = 2048
+PASSES = HID // K_PASS
+TOKEN_TILES = 4
+TOKENS = TOKEN_TILES * P
+CHUNK = 512
+CHUNKS = HID // CHUNK
+FEATURE_TILES = CHUNK // P
+RUN = 4
+VECTOR_COLS = 160
+LN_EPS = 1e-5
+LN_COLS = 1024
+
+FLOPS = 2 * 2 * TOKENS * HID * HID
+
+
+def tile_crossattentionlayer_pa_kernel(
+    tc, hidden_states, attn_ctx, Wo, bo, Wg, bg, ln_gamma, ln_beta, out
+):
+    nc = tc.nc
+    with ExitStack() as ctx:
+        const = ctx.enter_context(tc.tile_pool(name="const", bufs=1))
+        keep = ctx.enter_context(tc.tile_pool(name="keep", bufs=1))
+        raw_pool = ctx.enter_context(tc.tile_pool(name="raw", bufs=8))
+        stage = ctx.enter_context(tc.tile_pool(name="stage", bufs=4))
+        w_pool = ctx.enter_context(tc.tile_pool(name="w", bufs=2))
+        work = ctx.enter_context(tc.tile_pool(name="work", bufs=2))
+        psum_acc = ctx.enter_context(tc.psum_pool(name="psum_acc", bufs=2))
+        psum_t = ctx.enter_context(tc.psum_pool(name="psum_t", bufs=4))
+
+        h_rows = keep.tile([P, TOKEN_TILES, HID], BF16)
+        c_rows = keep.tile([P, TOKEN_TILES, HID], BF16)
+        for rows, source in ((h_rows, hidden_states), (c_rows, attn_ctx)):
+            for i in range(TOKEN_TILES):
+                nc.sync.dma_start(out=rows[:, i, :], in_=source[i])
+
+        ident_f32 = const.tile([P, P], F32)
+        make_identity(nc, ident_f32[:])
+        ident_bf16 = const.tile([P, P], BF16)
+        make_identity(nc, ident_bf16[:])
+
+        n_tiles = HID // P
+        bias_rows = const.tile([P, P], BF16)
+        nc.vector.memset(bias_rows[:], 0.0)
+        nc.sync.dma_start(out=bias_rows[0:n_tiles, :], in_=bo.rearrange("(c p) -> c p", p=P))
+        nc.sync.dma_start(out=bias_rows[n_tiles : 2 * n_tiles, :], in_=bg.rearrange("(c p) -> c p", p=P))
+        bias_t = psum_t.tile([P, P], BF16, tag="t")
+        nc.tensor.transpose(bias_t[:], bias_rows[:], ident_bf16[:])
+        bias_cols = const.tile([P, 2 * n_tiles], F32)
+        nc.vector.tensor_copy(out=bias_cols[:], in_=bias_t[:, 0 : 2 * n_tiles])
+
+        def quantise_activation(rows, codes, scales):
+            for pair in range(TOKEN_TILES // 2):
+                for g in range(PASSES):
+                    flipped = psum_t.tile([P, 2, 2 * P], F32, tag="t")
+                    for u in range(2):
+                        for s in range(2):
+                            words = rows[:, 2 * pair + s, :].bitcast(F32)
+                            nc.tensor.transpose(
+                                flipped[:, u, P * s : P * (s + 1)],
+                                words[:, 2 * P * g + u : 2 * P * (g + 1) : 2],
+                                ident_f32[:],
+                            )
+                    grouped = stage.tile([P, 2 * P * PACK], BF16, align_bytes=64, tag="x_grouped")
+                    side_by_side = grouped[:].bitcast(F32).rearrange("p (r u) -> p r u", u=2)
+                    if g % 2 == 0:
+                        nc.vector.tensor_copy(out=side_by_side, in_=flipped[:].rearrange("p u r -> p r u"))
+                    else:
+                        nc.scalar.copy(out=side_by_side, in_=flipped[:].rearrange("p u r -> p r u"))
+                    tokens = slice(2 * P * pair, 2 * P * (pair + 1))
+                    nc.vector.quantize_mx(
+                        out=codes[:, g, tokens].bitcast(FP8X4), scales=scales[:, g, tokens], in_=grouped[:]
+                    )
+
+        h_codes = keep.tile([P, PASSES, TOKENS], U32, align_bytes=64)
+        h_scales = keep.tile([P, PASSES, TOKENS], U8, align_bytes=64)
+        c_codes = keep.tile([P, PASSES, TOKENS], U32, align_bytes=64)
+        c_scales = keep.tile([P, PASSES, TOKENS], U8, align_bytes=64)
+        quantise_activation(h_rows, h_codes, h_scales)
+        quantise_activation(c_rows, c_codes, c_scales)
+
+        def regroup_weight_piece(w, g, cols):
+            raw = raw_pool.tile([P, PACK, CHUNK], BF16)
+            nc.sync.dma_start(
+                out=raw[:], in_=w[K_PASS * g : K_PASS * (g + 1), cols].rearrange("(p j) c -> p j c", j=PACK)
+            )
+            grouped = stage.tile([P, CHUNK, PACK], BF16, align_bytes=64, tag="w_grouped")
+            src = raw[:].rearrange("p j (c i) -> p c j i", i=RUN)
+            dst = grouped[:].rearrange("p (c i) j -> p c j i", i=RUN)
+            split = VECTOR_COLS // RUN
+            nc.vector.tensor_copy(out=dst[:, :split], in_=src[:, :split])
+            nc.scalar.copy(out=dst[:, split:], in_=src[:, split:])
+            return grouped
+
+        def quantise_weight_chunk(w, cols, codes, scales):
+            waiting = None
+            for g in range(PASSES + 1):
+                grouped = regroup_weight_piece(w, g, cols) if g < PASSES else None
+                if waiting is not None:
+                    nc.vector.quantize_mx(
+                        out=codes[:, g - 1, :].bitcast(FP8X4),
+                        scales=scales[:, g - 1, :],
+                        in_=waiting[:].rearrange("p c j -> p (c j)"),
+                    )
+                waiting = grouped
+
+        def product(acc, w_codes, w_scales, features, x_codes, x_scales):
+            for g in range(PASSES):
+                nc.tensor.matmul_mx(
+                    out=acc[:],
+                    lhsT=w_codes[:, g, features].bitcast(FP8X4),
+                    lhsT_scale=w_scales[:, g, features],
+                    rhs=x_codes[:, g, :].bitcast(FP8X4),
+                    rhs_scale=x_scales[:, g, :],
+                    start=(g == 0),
+                    stop=(g == PASSES - 1),
+                )
+
+        y = keep.tile([P, TOKEN_TILES, HID], F32)
+        stats = keep.tile([P, TOKEN_TILES, CHUNKS, 6], F32)
+        gamma_all = const.tile([P, HID], BF16)
+        beta_all = const.tile([P, HID], BF16)
+
+        for chunk in range(CHUNKS):
+            cols = slice(CHUNK * chunk, CHUNK * (chunk + 1))
+            wg_codes = w_pool.tile([P, PASSES, CHUNK], U32, align_bytes=64)
+            wg_scales = w_pool.tile([P, PASSES, CHUNK], U8, align_bytes=64)
+            wo_codes = w_pool.tile([P, PASSES, CHUNK], U32, align_bytes=64)
+            wo_scales = w_pool.tile([P, PASSES, CHUNK], U8, align_bytes=64)
+            quantise_weight_chunk(Wg, cols, wg_codes, wg_scales)
+            quantise_weight_chunk(Wo, cols, wo_codes, wo_scales)
+
+            if chunk == 0:
+                nc.sync.dma_start(out=gamma_all[:], in_=ln_gamma.partition_broadcast(P))
+                nc.sync.dma_start(out=beta_all[:], in_=ln_beta.partition_broadcast(P))
+
+            gated = work.tile([P, FEATURE_TILES, TOKENS], F32)
+            for f in range(FEATURE_TILES):
+                features = slice(P * f, P * (f + 1))
+                tile_index = FEATURE_TILES * chunk + f
+                acc_gate = psum_acc.tile([P, TOKENS], F32)
+                product(acc_gate, wg_codes, wg_scales, features, h_codes, h_scales)
+                acc_attn = psum_acc.tile([P, TOKENS], F32)
+                product(acc_attn, wo_codes, wo_scales, features, c_codes, c_scales)
+                gate = work.tile([P, TOKENS], F32)
+                nc.scalar.activation(
+                    out=gate[:],
+                    in_=acc_gate[:],
+                    func=ACT.Sigmoid,
+                    bias=bias_cols[:, n_tiles + tile_index : n_tiles + tile_index + 1],
+                    scale=1.0,
+                )
+                nc.vector.scalar_tensor_tensor(
+                    out=gated[:, f, :],
+                    in0=acc_attn[:],
+                    scalar=bias_cols[:, tile_index : tile_index + 1],
+                    in1=gate[:],
+                    op0=ALU.add,
+                    op1=ALU.mult,
+                )
+
+            for i in range(TOKEN_TILES):
+                back = psum_t.tile([P, CHUNK], F32, tag="t")
+                for f in range(FEATURE_TILES):
+                    nc.tensor.transpose(
+                        back[:, P * f : P * (f + 1)], gated[:, f, P * i : P * (i + 1)], ident_f32[:]
+                    )
+                nc.vector.tensor_tensor(out=y[:, i, cols], in0=back[:], in1=h_rows[:, i, cols], op=ALU.add)
+                nc.vector.bn_stats(out=stats[:, i, chunk, :], in_=y[:, i, cols])
+
+        mean_var = keep.tile([P, TOKEN_TILES, 2], F32)
+        for i in range(TOKEN_TILES):
+            nc.vector.bn_aggr(out=mean_var[:, i, :], in_=stats[:, i, :, :].rearrange("p c s -> p (c s)"))
+        rstd = keep.tile([P, TOKEN_TILES], F32)
+        nc.vector.tensor_scalar(out=rstd[:], in0=mean_var[:, :, 1], scalar1=LN_EPS, scalar2=None, op0=ALU.add)
+        nc.scalar.sqrt(out=rstd[:], in_=rstd[:])
+        nc.vector.reciprocal(out=rstd[:], in_=rstd[:])
+
+        out_rows = out.rearrange("b s d -> s b d")
+        for i in range(TOKEN_TILES):
+            for half in range(HID // LN_COLS):
+                cols = slice(LN_COLS * half, LN_COLS * (half + 1))
+                nc.vector.scalar_tensor_tensor(
+                    out=y[:, i, cols],
+                    in0=y[:, i, cols],
+                    scalar=mean_var[:, i, 0:1],
+                    in1=gamma_all[:, cols],
+                    op0=ALU.subtract,
+                    op1=ALU.mult,
+                )
+                nc.vector.scalar_tensor_tensor(
+                    out=y[:, i, cols],
+                    in0=y[:, i, cols],
+                    scalar=rstd[:, i : i + 1],
+                    in1=beta_all[:, cols],
+                    op0=ALU.mult,
+                    op1=ALU.add,
+                )
+                nc.sync.dma_start(out=out_rows[:, i, cols], in_=y[:, i, cols])

@@ -36,29 +36,30 @@ def tile_crossattentionlayer_pa_kernel(
     with ExitStack() as ctx:
         const = ctx.enter_context(tc.tile_pool(name="const", bufs=1))
         keep = ctx.enter_context(tc.tile_pool(name="keep", bufs=1))
-        raw_pool = ctx.enter_context(tc.tile_pool(name="raw", bufs=8))
+        raw_pool = ctx.enter_context(tc.tile_pool(name="raw", bufs=6))
         stage = ctx.enter_context(tc.tile_pool(name="stage", bufs=4))
-        w_pool = ctx.enter_context(tc.tile_pool(name="w", bufs=2))
+        w_pool = ctx.enter_context(tc.tile_pool(name="w", bufs=3))
         work = ctx.enter_context(tc.tile_pool(name="work", bufs=2))
         psum_acc = ctx.enter_context(tc.psum_pool(name="psum_acc", bufs=2))
-        psum_t = ctx.enter_context(tc.psum_pool(name="psum_t", bufs=4))
+        psum_t = ctx.enter_context(tc.psum_pool(name="psum_t", bufs=2))
+
+        n_tiles = HID // P
+        bias_rows = const.tile([P, P], BF16)
+        nc.vector.memset(bias_rows[:], 0.0)
+        nc.scalar.dma_start(out=bias_rows[0:n_tiles, :], in_=bo.rearrange("(c p) -> c p", p=P))
+        nc.scalar.dma_start(out=bias_rows[n_tiles : 2 * n_tiles, :], in_=bg.rearrange("(c p) -> c p", p=P))
 
         h_rows = keep.tile([P, TOKEN_TILES, HID], BF16)
         c_rows = keep.tile([P, TOKEN_TILES, HID], BF16)
         for rows, source in ((h_rows, hidden_states), (c_rows, attn_ctx)):
             for i in range(TOKEN_TILES):
-                nc.sync.dma_start(out=rows[:, i, :], in_=source[i])
+                nc.scalar.dma_start(out=rows[:, i, :], in_=source[i])
 
         ident_f32 = const.tile([P, P], F32)
         make_identity(nc, ident_f32[:])
         ident_bf16 = const.tile([P, P], BF16)
         make_identity(nc, ident_bf16[:])
 
-        n_tiles = HID // P
-        bias_rows = const.tile([P, P], BF16)
-        nc.vector.memset(bias_rows[:], 0.0)
-        nc.sync.dma_start(out=bias_rows[0:n_tiles, :], in_=bo.rearrange("(c p) -> c p", p=P))
-        nc.sync.dma_start(out=bias_rows[n_tiles : 2 * n_tiles, :], in_=bg.rearrange("(c p) -> c p", p=P))
         bias_t = psum_t.tile([P, P], BF16, tag="t")
         nc.tensor.transpose(bias_t[:], bias_rows[:], ident_bf16[:])
         bias_cols = const.tile([P, 2 * n_tiles], F32)
@@ -67,7 +68,7 @@ def tile_crossattentionlayer_pa_kernel(
         def quantise_activation(rows, codes, scales):
             for pair in range(TOKEN_TILES // 2):
                 for g in range(PASSES):
-                    flipped = psum_t.tile([P, 2, 2 * P], F32, tag="t")
+                    flipped = psum_acc.tile([P, 2, 2 * P], F32, tag="acc_attn", bufs=FEATURE_TILES)
                     for u in range(2):
                         for s in range(2):
                             words = rows[:, 2 * pair + s, :].bitcast(F32)
@@ -99,7 +100,7 @@ def tile_crossattentionlayer_pa_kernel(
             nc.sync.dma_start(
                 out=raw[:], in_=w[K_PASS * g : K_PASS * (g + 1), cols].rearrange("(p j) c -> p j c", j=PACK)
             )
-            grouped = stage.tile([P, CHUNK, PACK], BF16, align_bytes=64, tag="w_grouped")
+            grouped = stage.tile([P, CHUNK, PACK], BF16, align_bytes=64, tag="w_grouped", bufs=8)
             src = raw[:].rearrange("p j (c i) -> p c j i", i=RUN)
             dst = grouped[:].rearrange("p (c i) j -> p c j i", i=RUN)
             split = VECTOR_COLS // RUN
@@ -107,29 +108,29 @@ def tile_crossattentionlayer_pa_kernel(
             nc.scalar.copy(out=dst[:, split:], in_=src[:, split:])
             return grouped
 
-        def quantise_weight_chunk(w, cols, codes, scales):
-            waiting = None
-            for g in range(PASSES + 1):
-                grouped = regroup_weight_piece(w, g, cols) if g < PASSES else None
-                if waiting is not None:
-                    nc.vector.quantize_mx(
-                        out=codes[:, g - 1, :].bitcast(FP8X4),
-                        scales=scales[:, g - 1, :],
-                        in_=waiting[:].rearrange("p c j -> p (c j)"),
-                    )
-                waiting = grouped
-
-        def product(acc, w_codes, w_scales, features, x_codes, x_scales):
+        def quantise_weight_chunk(w, cols):
+            codes = w_pool.tile([P, PASSES, CHUNK], U32, align_bytes=64, tag="w_codes")
+            scales = w_pool.tile([P, PASSES, CHUNK], U8, align_bytes=64, tag="w_scales")
             for g in range(PASSES):
-                nc.tensor.matmul_mx(
-                    out=acc[:],
-                    lhsT=w_codes[:, g, features].bitcast(FP8X4),
-                    lhsT_scale=w_scales[:, g, features],
-                    rhs=x_codes[:, g, :].bitcast(FP8X4),
-                    rhs_scale=x_scales[:, g, :],
-                    start=(g == 0),
-                    stop=(g == PASSES - 1),
+                grouped = regroup_weight_piece(w, g, cols)
+                nc.vector.quantize_mx(
+                    out=codes[:, g, :].bitcast(FP8X4),
+                    scales=scales[:, g, :],
+                    in_=grouped[:].rearrange("p c j -> p (c j)"),
                 )
+            return codes, scales
+
+        def one_pass(acc, w_mx, f, x_mx, g):
+            features = slice(P * f, P * (f + 1))
+            nc.tensor.matmul_mx(
+                out=acc[:],
+                lhsT=w_mx[0][:, g, features].bitcast(FP8X4),
+                lhsT_scale=w_mx[1][:, g, features],
+                rhs=x_mx[0][:, g, :].bitcast(FP8X4),
+                rhs_scale=x_mx[1][:, g, :],
+                start=(g == 0),
+                stop=(g == PASSES - 1),
+            )
 
         y = keep.tile([P, TOKEN_TILES, HID], F32)
         stats = keep.tile([P, TOKEN_TILES, CHUNKS, 6], F32)
@@ -138,38 +139,38 @@ def tile_crossattentionlayer_pa_kernel(
 
         for chunk in range(CHUNKS):
             cols = slice(CHUNK * chunk, CHUNK * (chunk + 1))
-            wg_codes = w_pool.tile([P, PASSES, CHUNK], U32, align_bytes=64)
-            wg_scales = w_pool.tile([P, PASSES, CHUNK], U8, align_bytes=64)
-            wo_codes = w_pool.tile([P, PASSES, CHUNK], U32, align_bytes=64)
-            wo_scales = w_pool.tile([P, PASSES, CHUNK], U8, align_bytes=64)
-            quantise_weight_chunk(Wg, cols, wg_codes, wg_scales)
-            quantise_weight_chunk(Wo, cols, wo_codes, wo_scales)
+            first_tile = FEATURE_TILES * chunk
+            wg_mx = quantise_weight_chunk(Wg, cols)
+            wo_mx = quantise_weight_chunk(Wo, cols)
 
             if chunk == 0:
                 nc.sync.dma_start(out=gamma_all[:], in_=ln_gamma.partition_broadcast(P))
                 nc.sync.dma_start(out=beta_all[:], in_=ln_beta.partition_broadcast(P))
 
+            gate = work.tile([P, FEATURE_TILES, TOKENS], F32)
+            for f in range(FEATURE_TILES):
+                acc_gate = psum_acc.tile([P, TOKENS], F32)
+                for g in range(PASSES):
+                    one_pass(acc_gate, wg_mx, f, (h_codes, h_scales), g)
+                bg_col = n_tiles + first_tile + f
+                nc.scalar.activation(
+                    out=gate[:, f, :], in_=acc_gate[:], func=ACT.Sigmoid, bias=bias_cols[:, bg_col : bg_col + 1], scale=1.0
+                )
+
+            accs = [
+                psum_acc.tile([P, TOKENS], F32, name="acc_attn", bufs=FEATURE_TILES) for f in range(FEATURE_TILES)
+            ]
+            for g in range(PASSES):
+                for f in range(FEATURE_TILES):
+                    one_pass(accs[f], wo_mx, f, (c_codes, c_scales), g)
             gated = work.tile([P, FEATURE_TILES, TOKENS], F32)
             for f in range(FEATURE_TILES):
-                features = slice(P * f, P * (f + 1))
-                tile_index = FEATURE_TILES * chunk + f
-                acc_gate = psum_acc.tile([P, TOKENS], F32)
-                product(acc_gate, wg_codes, wg_scales, features, h_codes, h_scales)
-                acc_attn = psum_acc.tile([P, TOKENS], F32)
-                product(acc_attn, wo_codes, wo_scales, features, c_codes, c_scales)
-                gate = work.tile([P, TOKENS], F32)
-                nc.scalar.activation(
-                    out=gate[:],
-                    in_=acc_gate[:],
-                    func=ACT.Sigmoid,
-                    bias=bias_cols[:, n_tiles + tile_index : n_tiles + tile_index + 1],
-                    scale=1.0,
-                )
+                bo_col = first_tile + f
                 nc.vector.scalar_tensor_tensor(
                     out=gated[:, f, :],
-                    in0=acc_attn[:],
-                    scalar=bias_cols[:, tile_index : tile_index + 1],
-                    in1=gate[:],
+                    in0=accs[f][:],
+                    scalar=bias_cols[:, bo_col : bo_col + 1],
+                    in1=gate[:, f, :],
                     op0=ALU.add,
                     op1=ALU.mult,
                 )

@@ -36,30 +36,23 @@ def tile_crossattentionlayer_pa_kernel(
     with ExitStack() as ctx:
         const = ctx.enter_context(tc.tile_pool(name="const", bufs=1))
         keep = ctx.enter_context(tc.tile_pool(name="keep", bufs=1))
-        raw_pool = ctx.enter_context(tc.tile_pool(name="raw", bufs=6))
+        raw_pool = ctx.enter_context(tc.tile_pool(name="raw", bufs=8))
         stage = ctx.enter_context(tc.tile_pool(name="stage", bufs=4))
-        w_pool = ctx.enter_context(tc.tile_pool(name="w", bufs=3))
+        w_pool = ctx.enter_context(tc.tile_pool(name="w", bufs=4))
         work = ctx.enter_context(tc.tile_pool(name="work", bufs=2))
         psum_acc = ctx.enter_context(tc.psum_pool(name="psum_acc", bufs=2))
         psum_t = ctx.enter_context(tc.psum_pool(name="psum_t", bufs=2))
-
-        n_tiles = HID // P
-        bias_rows = const.tile([P, P], BF16)
-        nc.vector.memset(bias_rows[:], 0.0)
-        nc.scalar.dma_start(out=bias_rows[0:n_tiles, :], in_=bo.rearrange("(c p) -> c p", p=P))
-        nc.scalar.dma_start(out=bias_rows[n_tiles : 2 * n_tiles, :], in_=bg.rearrange("(c p) -> c p", p=P))
-
-        h_rows = keep.tile([P, TOKEN_TILES, HID], BF16)
-        c_rows = keep.tile([P, TOKEN_TILES, HID], BF16)
-        for rows, source in ((h_rows, hidden_states), (c_rows, attn_ctx)):
-            for i in range(TOKEN_TILES):
-                nc.scalar.dma_start(out=rows[:, i, :], in_=source[i])
 
         ident_f32 = const.tile([P, P], F32)
         make_identity(nc, ident_f32[:])
         ident_bf16 = const.tile([P, P], BF16)
         make_identity(nc, ident_bf16[:])
 
+        n_tiles = HID // P
+        bias_rows = const.tile([P, P], BF16)
+        nc.vector.memset(bias_rows[:], 0.0)
+        nc.scalar.dma_start(out=bias_rows[0:n_tiles, :], in_=bo.rearrange("(c p) -> c p", p=P))
+        nc.scalar.dma_start(out=bias_rows[n_tiles : 2 * n_tiles, :], in_=bg.rearrange("(c p) -> c p", p=P))
         bias_t = psum_t.tile([P, P], BF16, tag="t")
         nc.tensor.transpose(bias_t[:], bias_rows[:], ident_bf16[:])
         bias_cols = const.tile([P, 2 * n_tiles], F32)
@@ -92,15 +85,13 @@ def tile_crossattentionlayer_pa_kernel(
         h_scales = keep.tile([P, PASSES, TOKENS], U8, align_bytes=64)
         c_codes = keep.tile([P, PASSES, TOKENS], U32, align_bytes=64)
         c_scales = keep.tile([P, PASSES, TOKENS], U8, align_bytes=64)
-        quantise_activation(h_rows, h_codes, h_scales)
-        quantise_activation(c_rows, c_codes, c_scales)
 
         def regroup_weight_piece(w, g, cols):
             raw = raw_pool.tile([P, PACK, CHUNK], BF16)
             nc.sync.dma_start(
                 out=raw[:], in_=w[K_PASS * g : K_PASS * (g + 1), cols].rearrange("(p j) c -> p j c", j=PACK)
             )
-            grouped = stage.tile([P, CHUNK, PACK], BF16, align_bytes=64, tag="w_grouped", bufs=8)
+            grouped = stage.tile([P, CHUNK, PACK], BF16, align_bytes=64, tag="w_grouped")
             src = raw[:].rearrange("p j (c i) -> p c j i", i=RUN)
             dst = grouped[:].rearrange("p (c i) j -> p c j i", i=RUN)
             split = VECTOR_COLS // RUN
@@ -132,6 +123,8 @@ def tile_crossattentionlayer_pa_kernel(
                 stop=(g == PASSES - 1),
             )
 
+        h_rows = keep.tile([P, TOKEN_TILES, HID], BF16)
+        c_rows = keep.tile([P, TOKEN_TILES, HID], BF16)
         y = keep.tile([P, TOKEN_TILES, HID], F32)
         stats = keep.tile([P, TOKEN_TILES, CHUNKS, 6], F32)
         gamma_all = const.tile([P, HID], BF16)
@@ -144,6 +137,11 @@ def tile_crossattentionlayer_pa_kernel(
             wo_mx = quantise_weight_chunk(Wo, cols)
 
             if chunk == 0:
+                for rows, source in ((h_rows, hidden_states), (c_rows, attn_ctx)):
+                    for i in range(TOKEN_TILES):
+                        nc.sync.dma_start(out=rows[:, i, :], in_=source[i])
+                quantise_activation(h_rows, h_codes, h_scales)
+                quantise_activation(c_rows, c_codes, c_scales)
                 nc.sync.dma_start(out=gamma_all[:], in_=ln_gamma.partition_broadcast(P))
                 nc.sync.dma_start(out=beta_all[:], in_=ln_beta.partition_broadcast(P))
 

@@ -58,6 +58,12 @@ def tile_crossattentionlayer_pa_kernel(
         bias_cols = const.tile([P, 2 * n_tiles], F32)
         nc.vector.tensor_copy(out=bias_cols[:], in_=bias_t[:, 0 : 2 * n_tiles])
 
+        norm_rows = const.tile([P, HID], BF16)
+        nc.gpsimd.memset(norm_rows[:], 0.0)
+        shift_cols = const.tile([P, TOKEN_TILES, P], BF16)
+        nc.vector.memset(shift_cols[:], 0.0)
+        nc.vector.memset(shift_cols[:, :, 2:3], 1.0)
+
         def quantise_activation(rows, codes, scales):
             for pair in range(TOKEN_TILES // 2):
                 for g in range(PASSES):
@@ -125,10 +131,9 @@ def tile_crossattentionlayer_pa_kernel(
 
         h_rows = keep.tile([P, TOKEN_TILES, HID], BF16)
         c_rows = keep.tile([P, TOKEN_TILES, HID], BF16)
-        y = keep.tile([P, TOKEN_TILES, HID], F32)
+        y_gamma = keep.tile([P, TOKEN_TILES, HID], F32)
         stats = keep.tile([P, TOKEN_TILES, CHUNKS, 6], F32)
         gamma_all = const.tile([P, HID], BF16)
-        beta_all = const.tile([P, HID], BF16)
 
         for chunk in range(CHUNKS):
             cols = slice(CHUNK * chunk, CHUNK * (chunk + 1))
@@ -143,7 +148,9 @@ def tile_crossattentionlayer_pa_kernel(
                 quantise_activation(h_rows, h_codes, h_scales)
                 quantise_activation(c_rows, c_codes, c_scales)
                 nc.sync.dma_start(out=gamma_all[:], in_=ln_gamma.partition_broadcast(P))
-                nc.sync.dma_start(out=beta_all[:], in_=ln_beta.partition_broadcast(P))
+                nc.sync.dma_start(out=norm_rows[0:1, :], in_=ln_gamma.unsqueeze(0))
+                nc.sync.dma_start(out=norm_rows[1:2, :], in_=ln_gamma.unsqueeze(0))
+                nc.sync.dma_start(out=norm_rows[2:3, :], in_=ln_beta.unsqueeze(0))
 
             gate = work.tile([P, FEATURE_TILES, TOKENS], F32)
             for f in range(FEATURE_TILES):
@@ -175,12 +182,21 @@ def tile_crossattentionlayer_pa_kernel(
 
             for i in range(TOKEN_TILES):
                 back = psum_t.tile([P, CHUNK], F32, tag="t")
+                nc.tensor.matmul(back[:], lhsT=ident_bf16[:], rhs=h_rows[:, i, cols], start=True, stop=False)
                 for f in range(FEATURE_TILES):
-                    nc.tensor.transpose(
-                        back[:, P * f : P * (f + 1)], gated[:, f, P * i : P * (i + 1)], ident_f32[:]
+                    nc.tensor.matmul(
+                        back[:, P * f : P * (f + 1)],
+                        lhsT=gated[:, f, P * i : P * (i + 1)],
+                        rhs=ident_f32[:],
+                        is_transpose=True,
+                        start=False,
+                        stop=(f == FEATURE_TILES - 1),
                     )
-                nc.vector.tensor_tensor(out=y[:, i, cols], in0=back[:], in1=h_rows[:, i, cols], op=ALU.add)
-                nc.vector.bn_stats(out=stats[:, i, chunk, :], in_=y[:, i, cols])
+                nc.vector.bn_stats(out=stats[:, i, chunk, :], in_=back[:])
+                nc.vector.tensor_tensor(out=y_gamma[:, i, cols], in0=back[:], in1=gamma_all[:, cols], op=ALU.mult)
+
+        sqrt_warm = const.tile([P, 1], F32)
+        nc.scalar.sqrt(out=sqrt_warm[:], in_=gate[:, FEATURE_TILES - 1, 0:1])
 
         mean_var = keep.tile([P, TOKEN_TILES, 2], F32)
         for i in range(TOKEN_TILES):
@@ -190,24 +206,34 @@ def tile_crossattentionlayer_pa_kernel(
         nc.scalar.sqrt(out=rstd[:], in_=rstd[:])
         nc.vector.reciprocal(out=rstd[:], in_=rstd[:])
 
+        shift = keep.tile([P, TOKEN_TILES], F32)
+        nc.vector.scalar_tensor_tensor(
+            out=shift[:], in0=mean_var[:, :, 0], scalar=-1.0, in1=rstd[:], op0=ALU.mult, op1=ALU.mult
+        )
+        nc.vector.tensor_copy(out=shift_cols[:, :, 0], in_=shift[:])
+        nc.vector.tensor_tensor(out=shift_cols[:, :, 1], in0=shift[:], in1=shift_cols[:, :, 0], op=ALU.subtract)
+        shift_t = psum_t.tile([P, TOKENS], BF16, tag="t")
+        for i in range(TOKEN_TILES):
+            nc.tensor.transpose(shift_t[:, P * i : P * (i + 1)], shift_cols[:, i, :], ident_bf16[:])
+        shift_rows = keep.tile([P, TOKENS], BF16)
+        nc.scalar.copy(out=shift_rows[:], in_=shift_t[:])
+
         out_rows = out.rearrange("b s d -> s b d")
         for i in range(TOKEN_TILES):
             for half in range(HID // LN_COLS):
+                for c in range(LN_COLS // CHUNK):
+                    cols = slice(LN_COLS * half + CHUNK * c, LN_COLS * half + CHUNK * (c + 1))
+                    offset = psum_acc.tile([P, CHUNK], F32, tag="acc_attn", bufs=FEATURE_TILES)
+                    nc.tensor.matmul(
+                        offset[:], lhsT=shift_rows[:, P * i : P * (i + 1)], rhs=norm_rows[:, cols], start=True, stop=True
+                    )
+                    nc.vector.scalar_tensor_tensor(
+                        out=y_gamma[:, i, cols],
+                        in0=y_gamma[:, i, cols],
+                        scalar=rstd[:, i : i + 1],
+                        in1=offset[:],
+                        op0=ALU.mult,
+                        op1=ALU.add,
+                    )
                 cols = slice(LN_COLS * half, LN_COLS * (half + 1))
-                nc.vector.scalar_tensor_tensor(
-                    out=y[:, i, cols],
-                    in0=y[:, i, cols],
-                    scalar=mean_var[:, i, 0:1],
-                    in1=gamma_all[:, cols],
-                    op0=ALU.subtract,
-                    op1=ALU.mult,
-                )
-                nc.vector.scalar_tensor_tensor(
-                    out=y[:, i, cols],
-                    in0=y[:, i, cols],
-                    scalar=rstd[:, i : i + 1],
-                    in1=beta_all[:, cols],
-                    op0=ALU.mult,
-                    op1=ALU.add,
-                )
-                nc.sync.dma_start(out=out_rows[:, i, cols], in_=y[:, i, cols])
+                nc.sync.dma_start(out=out_rows[:, i, cols], in_=y_gamma[:, i, cols])

@@ -22,7 +22,9 @@ CHUNK = 512
 CHUNKS = HID // CHUNK
 FEATURE_TILES = CHUNK // P
 RUN = 4
-VECTOR_COLS = 160
+PIECES = CHUNKS * 2 * PASSES
+CHUNK_PIECES = 2 * PASSES
+VECTOR_COLS = (192, 192, 192, 128)
 LN_EPS = 1e-5
 LN_COLS = 1024
 
@@ -37,166 +39,272 @@ def tile_crossattentionlayer_pa_kernel(
         const = ctx.enter_context(tc.tile_pool(name="const", bufs=1))
         keep = ctx.enter_context(tc.tile_pool(name="keep", bufs=1))
         raw_pool = ctx.enter_context(tc.tile_pool(name="raw", bufs=8))
-        stage = ctx.enter_context(tc.tile_pool(name="stage", bufs=4))
+        stage = ctx.enter_context(tc.tile_pool(name="stage", bufs=5))
         w_pool = ctx.enter_context(tc.tile_pool(name="w", bufs=4))
         work = ctx.enter_context(tc.tile_pool(name="work", bufs=2))
-        psum_acc = ctx.enter_context(tc.psum_pool(name="psum_acc", bufs=2))
-        psum_t = ctx.enter_context(tc.psum_pool(name="psum_t", bufs=2))
+        psum_acc = ctx.enter_context(tc.psum_pool(name="psum_acc", bufs=5))
+        psum_t = ctx.enter_context(tc.psum_pool(name="psum_t", bufs=3))
+        ctx.enter_context(tc.manual_schedule())
+
+        h_rows = keep.tile([P, TOKEN_TILES, HID], BF16)
+        c_rows = keep.tile([P, TOKEN_TILES, HID], BF16)
+        h_codes = keep.tile([P, PASSES, TOKENS], U32, align_bytes=64)
+        h_scales = keep.tile([P, PASSES, TOKENS], U8, align_bytes=64)
+        c_codes = keep.tile([P, PASSES, TOKENS], U32, align_bytes=64)
+        c_scales = keep.tile([P, PASSES, TOKENS], U8, align_bytes=64)
+        y_gamma = keep.tile([P, TOKEN_TILES, HID], F32)
+        stats = keep.tile([P, TOKEN_TILES, CHUNKS, 6], F32)
+        gamma_all = const.tile([P, HID], BF16)
 
         ident_f32 = const.tile([P, P], F32)
         make_identity(nc, ident_f32[:])
         ident_bf16 = const.tile([P, P], BF16)
         make_identity(nc, ident_bf16[:])
+        norm_rows = const.tile([P, HID], BF16)
+        nc.gpsimd.memset(norm_rows[:], 0.0)
 
         n_tiles = HID // P
         bias_rows = const.tile([P, P], BF16)
         nc.vector.memset(bias_rows[:], 0.0)
         nc.scalar.dma_start(out=bias_rows[0:n_tiles, :], in_=bo.rearrange("(c p) -> c p", p=P))
         nc.scalar.dma_start(out=bias_rows[n_tiles : 2 * n_tiles, :], in_=bg.rearrange("(c p) -> c p", p=P))
-        bias_t = psum_t.tile([P, P], BF16, tag="t")
-        nc.tensor.transpose(bias_t[:], bias_rows[:], ident_bf16[:])
-        bias_cols = const.tile([P, 2 * n_tiles], F32)
-        nc.vector.tensor_copy(out=bias_cols[:], in_=bias_t[:, 0 : 2 * n_tiles])
-
-        norm_rows = const.tile([P, HID], BF16)
-        nc.gpsimd.memset(norm_rows[:], 0.0)
         shift_cols = const.tile([P, TOKEN_TILES, P], BF16)
         nc.vector.memset(shift_cols[:], 0.0)
         nc.vector.memset(shift_cols[:, :, 2:3], 1.0)
+        bias_cols = const.tile([P, 2 * n_tiles], F32)
 
-        def quantise_activation(rows, codes, scales):
-            for pair in range(TOKEN_TILES // 2):
-                for g in range(PASSES):
-                    flipped = psum_acc.tile([P, 2, 2 * P], F32, tag="acc_attn", bufs=FEATURE_TILES)
-                    for u in range(2):
-                        for s in range(2):
-                            words = rows[:, 2 * pair + s, :].bitcast(F32)
-                            nc.tensor.transpose(
-                                flipped[:, u, P * s : P * (s + 1)],
-                                words[:, 2 * P * g + u : 2 * P * (g + 1) : 2],
-                                ident_f32[:],
-                            )
-                    grouped = stage.tile([P, 2 * P * PACK], BF16, align_bytes=64, tag="x_grouped")
-                    side_by_side = grouped[:].bitcast(F32).rearrange("p (r u) -> p r u", u=2)
-                    if g % 2 == 0:
-                        nc.vector.tensor_copy(out=side_by_side, in_=flipped[:].rearrange("p u r -> p r u"))
-                    else:
-                        nc.scalar.copy(out=side_by_side, in_=flipped[:].rearrange("p u r -> p r u"))
-                    tokens = slice(2 * P * pair, 2 * P * (pair + 1))
-                    nc.vector.quantize_mx(
-                        out=codes[:, g, tokens].bitcast(FP8X4), scales=scales[:, g, tokens], in_=grouped[:]
-                    )
+        def make_bias_cols():
+            bias_t = psum_t.tile([P, P], BF16, name="t")
+            nc.tensor.transpose(bias_t[:], bias_rows[:], ident_bf16[:])
+            nc.vector.tensor_copy(out=bias_cols[:], in_=bias_t[:, 0 : 2 * n_tiles])
 
-        h_codes = keep.tile([P, PASSES, TOKENS], U32, align_bytes=64)
-        h_scales = keep.tile([P, PASSES, TOKENS], U8, align_bytes=64)
-        c_codes = keep.tile([P, PASSES, TOKENS], U32, align_bytes=64)
-        c_scales = keep.tile([P, PASSES, TOKENS], U8, align_bytes=64)
+        def piece_of(n):
+            chunk, rest = divmod(n, CHUNK_PIECES)
+            which, g = divmod(rest, PASSES)
+            return which, g, slice(CHUNK * chunk, CHUNK * (chunk + 1))
 
-        def regroup_weight_piece(w, g, cols):
-            raw = raw_pool.tile([P, PACK, CHUNK], BF16)
+        raws = {}
+
+        def load_piece(n):
+            which, g, cols = piece_of(n)
+            raw = raw_pool.tile([P, PACK, CHUNK], BF16, name="raw")
+            w = (Wg, Wo)[which]
             nc.sync.dma_start(
                 out=raw[:], in_=w[K_PASS * g : K_PASS * (g + 1), cols].rearrange("(p j) c -> p j c", j=PACK)
             )
-            grouped = stage.tile([P, CHUNK, PACK], BF16, align_bytes=64, tag="w_grouped")
+            raws[n] = raw
+
+        def load_tokens(rows, source, i):
+            nc.sync.dma_start(out=rows[:, i, :], in_=source[i])
+
+        for i in range(TOKEN_TILES):
+            load_piece(i)
+            if i == 1:
+                load_tokens(h_rows, hidden_states, 0)
+                load_tokens(h_rows, hidden_states, 1)
+            if i > 1:
+                load_tokens(h_rows, hidden_states, i)
+        for i in range(TOKEN_TILES):
+            load_piece(TOKEN_TILES + i)
+            load_tokens(c_rows, attn_ctx, i)
+
+        groupeds = {}
+        w_mx = {}
+
+        def regroup_piece(n):
+            raw = raws.pop(n)
+            grouped = stage.tile([P, CHUNK, PACK], BF16, align_bytes=64, name="w_grouped")
             src = raw[:].rearrange("p j (c i) -> p c j i", i=RUN)
             dst = grouped[:].rearrange("p (c i) j -> p c j i", i=RUN)
-            split = VECTOR_COLS // RUN
-            nc.vector.tensor_copy(out=dst[:, :split], in_=src[:, :split])
+            split = VECTOR_COLS[n // CHUNK_PIECES] // RUN
             nc.scalar.copy(out=dst[:, split:], in_=src[:, split:])
-            return grouped
+            if split:
+                nc.vector.tensor_copy(out=dst[:, :split], in_=src[:, :split])
+            groupeds[n] = grouped
 
-        def quantise_weight_chunk(w, cols):
-            codes = w_pool.tile([P, PASSES, CHUNK], U32, align_bytes=64, tag="w_codes")
-            scales = w_pool.tile([P, PASSES, CHUNK], U8, align_bytes=64, tag="w_scales")
-            for g in range(PASSES):
-                grouped = regroup_weight_piece(w, g, cols)
-                nc.vector.quantize_mx(
-                    out=codes[:, g, :].bitcast(FP8X4),
-                    scales=scales[:, g, :],
-                    in_=grouped[:].rearrange("p c j -> p (c j)"),
-                )
-            return codes, scales
+        def quantise_piece(n):
+            g = n % PASSES
+            if g == 0:
+                codes = w_pool.tile([P, PASSES, CHUNK], U32, align_bytes=64, name="w_codes")
+                scales = w_pool.tile([P, PASSES, CHUNK], U8, align_bytes=64, name="w_scales")
+                w_mx[n // PASSES] = (codes, scales)
+            codes, scales = w_mx[n // PASSES]
+            nc.vector.quantize_mx(
+                out=codes[:, g, :].bitcast(FP8X4),
+                scales=scales[:, g, :],
+                in_=groupeds.pop(n)[:].rearrange("p c j -> p (c j)"),
+            )
 
-        def one_pass(acc, w_mx, f, x_mx, g):
+        units = [(m, pair, g) for m in range(2) for pair in range(TOKEN_TILES // 2) for g in range(PASSES)]
+        flips = {}
+        x_grouped = {}
+
+        def flip_unit(k):
+            m, pair, g = units[k]
+            rows = (h_rows, c_rows)[m]
+            flipped = psum_t.tile([P, 2, 2 * P], F32, name="t")
+            for u in range(2):
+                for s in range(2):
+                    words = rows[:, 2 * pair + s, :].bitcast(F32)
+                    nc.tensor.transpose(
+                        flipped[:, u, P * s : P * (s + 1)], words[:, 2 * P * g + u : 2 * P * (g + 1) : 2], ident_f32[:]
+                    )
+            flips[k] = flipped
+
+        def group_unit(k):
+            flipped = flips.pop(k)
+            grouped = stage.tile([P, 2 * P * PACK], BF16, align_bytes=64, name="x_grouped")
+            side_by_side = grouped[:].bitcast(F32).rearrange("p (r u) -> p r u", u=2)
+            if k % 2 == 0:
+                nc.vector.tensor_copy(out=side_by_side, in_=flipped[:].rearrange("p u r -> p r u"))
+            else:
+                nc.scalar.copy(out=side_by_side, in_=flipped[:].rearrange("p u r -> p r u"))
+            x_grouped[k] = grouped
+
+        def quantise_unit(k):
+            m, pair, g = units[k]
+            codes, scales = ((h_codes, h_scales), (c_codes, c_scales))[m]
+            tokens = slice(2 * P * pair, 2 * P * (pair + 1))
+            nc.vector.quantize_mx(
+                out=codes[:, g, tokens].bitcast(FP8X4), scales=scales[:, g, tokens], in_=x_grouped.pop(k)[:]
+            )
+
+        gates = {}
+        accs = {}
+
+        def one_pass(acc, w, f, x_mx, g):
             features = slice(P * f, P * (f + 1))
             nc.tensor.matmul_mx(
                 out=acc[:],
-                lhsT=w_mx[0][:, g, features].bitcast(FP8X4),
-                lhsT_scale=w_mx[1][:, g, features],
+                lhsT=w[0][:, g, features].bitcast(FP8X4),
+                lhsT_scale=w[1][:, g, features],
                 rhs=x_mx[0][:, g, :].bitcast(FP8X4),
                 rhs_scale=x_mx[1][:, g, :],
                 start=(g == 0),
                 stop=(g == PASSES - 1),
             )
 
-        h_rows = keep.tile([P, TOKEN_TILES, HID], BF16)
-        c_rows = keep.tile([P, TOKEN_TILES, HID], BF16)
-        y_gamma = keep.tile([P, TOKEN_TILES, HID], F32)
-        stats = keep.tile([P, TOKEN_TILES, CHUNKS, 6], F32)
-        gamma_all = const.tile([P, HID], BF16)
+        def product(which, chunk, f):
+            acc = psum_acc.tile([P, TOKENS], F32, name="acc")
+            x_mx = ((h_codes, h_scales), (c_codes, c_scales))[which]
+            for g in range(PASSES):
+                one_pass(acc, w_mx[2 * chunk + which], f, x_mx, g)
+            accs[which, chunk, f] = acc
 
-        for chunk in range(CHUNKS):
+        def product_pass(chunk, g):
+            for f in range(FEATURE_TILES):
+                if g == 0:
+                    accs[1, chunk, f] = psum_acc.tile([P, TOKENS], F32, name="acc")
+                one_pass(accs[1, chunk, f], w_mx[2 * chunk + 1], f, (c_codes, c_scales), g)
+
+        def sigmoid(chunk, f):
+            if f == 0:
+                gates[chunk] = work.tile([P, FEATURE_TILES, TOKENS], F32, name="gate")
+            bg_col = n_tiles + FEATURE_TILES * chunk + f
+            nc.scalar.activation(
+                out=gates[chunk][:, f, :],
+                in_=accs.pop((0, chunk, f))[:],
+                func=ACT.Sigmoid,
+                bias=bias_cols[:, bg_col : bg_col + 1],
+                scale=1.0,
+            )
+
+        def apply_gate(chunk, f):
+            bo_col = FEATURE_TILES * chunk + f
+            gate = gates[chunk]
+            nc.vector.scalar_tensor_tensor(
+                out=gate[:, f, :],
+                in0=accs.pop((1, chunk, f))[:],
+                scalar=bias_cols[:, bo_col : bo_col + 1],
+                in1=gate[:, f, :],
+                op0=ALU.add,
+                op1=ALU.mult,
+            )
+
+        backs = {}
+
+        def back_to_tokens(chunk, i):
             cols = slice(CHUNK * chunk, CHUNK * (chunk + 1))
-            first_tile = FEATURE_TILES * chunk
-            wg_mx = quantise_weight_chunk(Wg, cols)
-            wo_mx = quantise_weight_chunk(Wo, cols)
+            if chunk == CHUNKS - 1:
+                back = psum_acc.tile([P, CHUNK], F32, name="acc")
+            else:
+                back = psum_t.tile([P, CHUNK], F32, name="t")
+            nc.tensor.matmul(back[:], lhsT=ident_bf16[:], rhs=h_rows[:, i, cols], start=True, stop=False)
+            for f in range(FEATURE_TILES):
+                nc.tensor.matmul(
+                    back[:, P * f : P * (f + 1)],
+                    lhsT=gates[chunk][:, f, P * i : P * (i + 1)],
+                    rhs=ident_f32[:],
+                    is_transpose=True,
+                    start=False,
+                    stop=(f == FEATURE_TILES - 1),
+                )
+            backs[chunk, i] = back
 
-            if chunk == 0:
-                for rows, source in ((h_rows, hidden_states), (c_rows, attn_ctx)):
-                    for i in range(TOKEN_TILES):
-                        nc.sync.dma_start(out=rows[:, i, :], in_=source[i])
-                quantise_activation(h_rows, h_codes, h_scales)
-                quantise_activation(c_rows, c_codes, c_scales)
+        def take_stats(chunk, i):
+            nc.vector.bn_stats(out=stats[:, i, chunk, :], in_=backs[chunk, i][:])
+
+        def take_y(chunk, i):
+            cols = slice(CHUNK * chunk, CHUNK * (chunk + 1))
+            nc.vector.tensor_tensor(out=y_gamma[:, i, cols], in0=backs.pop((chunk, i))[:], in1=gamma_all[:, cols], op=ALU.mult)
+
+        last = CHUNKS - 1
+        for s in range(PIECES + 1):
+            if s == 1:
                 nc.sync.dma_start(out=gamma_all[:], in_=ln_gamma.partition_broadcast(P))
                 nc.sync.dma_start(out=norm_rows[0:1, :], in_=ln_gamma.unsqueeze(0))
                 nc.sync.dma_start(out=norm_rows[1:2, :], in_=ln_gamma.unsqueeze(0))
                 nc.sync.dma_start(out=norm_rows[2:3, :], in_=ln_beta.unsqueeze(0))
+                make_bias_cols()
+            for chunk in range(CHUNKS):
+                t = s - CHUNK_PIECES * chunk
+                if 6 <= t < 10:
+                    sigmoid(chunk, t - 6)
+                if 10 <= t < 14 and chunk != last:
+                    apply_gate(chunk, t - 10)
+                if 15 <= t < 17:
+                    for i in (2 * (t - 15), 2 * (t - 15) + 1):
+                        take_stats(chunk, i)
+                        take_y(chunk, i)
+            if s < PIECES:
+                regroup_piece(s)
+            ahead = s + 2 * TOKEN_TILES
+            if ahead < PIECES:
+                load_piece(ahead)
+            if s >= 1:
+                quantise_piece(s - 1)
+            first = 2 * (s - 2)
+            if s % 2 == 0 and 0 <= first < len(units):
+                for k in (first, first + 2):
+                    flip_unit(k)
+                    flip_unit(k + 1)
+                    group_unit(k)
+                    group_unit(k + 1)
+            first = 2 * (s - 3)
+            if s % 2 == 1 and 0 <= first < len(units):
+                for k in range(first, first + PASSES):
+                    quantise_unit(k)
+            for chunk in range(CHUNKS):
+                t = s - CHUNK_PIECES * chunk
+                if 5 <= t < 9:
+                    product(0, chunk, t - 5)
+                if 9 <= t < 13 and chunk != last:
+                    product(1, chunk, t - 9)
+                if chunk == last and 5 <= t:
+                    product_pass(chunk, t - 5)
+                if 14 <= t < 16:
+                    for i in (2 * (t - 14), 2 * (t - 14) + 1):
+                        back_to_tokens(chunk, i)
 
-            gate = work.tile([P, FEATURE_TILES, TOKENS], F32)
-            for f in range(FEATURE_TILES):
-                acc_gate = psum_acc.tile([P, TOKENS], F32)
-                for g in range(PASSES):
-                    one_pass(acc_gate, wg_mx, f, (h_codes, h_scales), g)
-                bg_col = n_tiles + first_tile + f
-                nc.scalar.activation(
-                    out=gate[:, f, :], in_=acc_gate[:], func=ACT.Sigmoid, bias=bias_cols[:, bg_col : bg_col + 1], scale=1.0
-                )
-
-            accs = [
-                psum_acc.tile([P, TOKENS], F32, name="acc_attn", bufs=FEATURE_TILES) for f in range(FEATURE_TILES)
-            ]
-            for g in range(PASSES):
-                for f in range(FEATURE_TILES):
-                    one_pass(accs[f], wo_mx, f, (c_codes, c_scales), g)
-            gated = work.tile([P, FEATURE_TILES, TOKENS], F32)
-            for f in range(FEATURE_TILES):
-                bo_col = first_tile + f
-                nc.vector.scalar_tensor_tensor(
-                    out=gated[:, f, :],
-                    in0=accs[f][:],
-                    scalar=bias_cols[:, bo_col : bo_col + 1],
-                    in1=gate[:, f, :],
-                    op0=ALU.add,
-                    op1=ALU.mult,
-                )
-
-            for i in range(TOKEN_TILES):
-                back = psum_t.tile([P, CHUNK], F32, tag="t")
-                nc.tensor.matmul(back[:], lhsT=ident_bf16[:], rhs=h_rows[:, i, cols], start=True, stop=False)
-                for f in range(FEATURE_TILES):
-                    nc.tensor.matmul(
-                        back[:, P * f : P * (f + 1)],
-                        lhsT=gated[:, f, P * i : P * (i + 1)],
-                        rhs=ident_f32[:],
-                        is_transpose=True,
-                        start=False,
-                        stop=(f == FEATURE_TILES - 1),
-                    )
-                nc.vector.bn_stats(out=stats[:, i, chunk, :], in_=back[:])
-                nc.vector.tensor_tensor(out=y_gamma[:, i, cols], in0=back[:], in1=gamma_all[:, cols], op=ALU.mult)
-
+        sigmoid(last, 3)
         sqrt_warm = const.tile([P, 1], F32)
-        nc.scalar.sqrt(out=sqrt_warm[:], in_=gate[:, FEATURE_TILES - 1, 0:1])
+        nc.scalar.sqrt(out=sqrt_warm[:], in_=gates[last][:, 3, 0:1])
+        for f in range(FEATURE_TILES):
+            apply_gate(last, f)
+        for i in range(TOKEN_TILES):
+            back_to_tokens(last, i)
+        for i in range(TOKEN_TILES):
+            take_stats(last, i)
 
         mean_var = keep.tile([P, TOKEN_TILES, 2], F32)
         for i in range(TOKEN_TILES):
@@ -204,15 +312,17 @@ def tile_crossattentionlayer_pa_kernel(
         rstd = keep.tile([P, TOKEN_TILES], F32)
         nc.vector.tensor_scalar(out=rstd[:], in0=mean_var[:, :, 1], scalar1=LN_EPS, scalar2=None, op0=ALU.add)
         nc.scalar.sqrt(out=rstd[:], in_=rstd[:])
+        take_y(last, 0)
         nc.vector.reciprocal(out=rstd[:], in_=rstd[:])
-
         shift = keep.tile([P, TOKEN_TILES], F32)
         nc.vector.scalar_tensor_tensor(
             out=shift[:], in0=mean_var[:, :, 0], scalar=-1.0, in1=rstd[:], op0=ALU.mult, op1=ALU.mult
         )
         nc.vector.tensor_copy(out=shift_cols[:, :, 0], in_=shift[:])
         nc.vector.tensor_tensor(out=shift_cols[:, :, 1], in0=shift[:], in1=shift_cols[:, :, 0], op=ALU.subtract)
-        shift_t = psum_t.tile([P, TOKENS], BF16, tag="t")
+        for i in range(1, TOKEN_TILES):
+            take_y(last, i)
+        shift_t = psum_t.tile([P, TOKENS], BF16, name="t")
         for i in range(TOKEN_TILES):
             nc.tensor.transpose(shift_t[:, P * i : P * (i + 1)], shift_cols[:, i, :], ident_bf16[:])
         shift_rows = keep.tile([P, TOKENS], BF16)
@@ -220,20 +330,20 @@ def tile_crossattentionlayer_pa_kernel(
 
         out_rows = out.rearrange("b s d -> s b d")
         for i in range(TOKEN_TILES):
-            for half in range(HID // LN_COLS):
-                for c in range(LN_COLS // CHUNK):
-                    cols = slice(LN_COLS * half + CHUNK * c, LN_COLS * half + CHUNK * (c + 1))
-                    offset = psum_acc.tile([P, CHUNK], F32, tag="acc_attn", bufs=FEATURE_TILES)
-                    nc.tensor.matmul(
-                        offset[:], lhsT=shift_rows[:, P * i : P * (i + 1)], rhs=norm_rows[:, cols], start=True, stop=True
-                    )
-                    nc.vector.scalar_tensor_tensor(
-                        out=y_gamma[:, i, cols],
-                        in0=y_gamma[:, i, cols],
-                        scalar=rstd[:, i : i + 1],
-                        in1=offset[:],
-                        op0=ALU.mult,
-                        op1=ALU.add,
-                    )
-                cols = slice(LN_COLS * half, LN_COLS * (half + 1))
-                nc.sync.dma_start(out=out_rows[:, i, cols], in_=y_gamma[:, i, cols])
+            for c in range(CHUNKS):
+                cols = slice(CHUNK * c, CHUNK * (c + 1))
+                offset = psum_acc.tile([P, CHUNK], F32, name="acc")
+                nc.tensor.matmul(
+                    offset[:], lhsT=shift_rows[:, P * i : P * (i + 1)], rhs=norm_rows[:, cols], start=True, stop=True
+                )
+                nc.vector.scalar_tensor_tensor(
+                    out=y_gamma[:, i, cols],
+                    in0=y_gamma[:, i, cols],
+                    scalar=rstd[:, i : i + 1],
+                    in1=offset[:],
+                    op0=ALU.mult,
+                    op1=ALU.add,
+                )
+                if (c + 1) * CHUNK % LN_COLS == 0:
+                    cols = slice((c + 1) * CHUNK - LN_COLS, (c + 1) * CHUNK)
+                    nc.sync.dma_start(out=out_rows[:, i, cols], in_=y_gamma[:, i, cols])

@@ -1,4 +1,5 @@
 from contextlib import ExitStack
+from functools import partial
 
 import concourse.mybir as mybir
 from concourse.masks import make_identity
@@ -25,6 +26,15 @@ RUN = 4
 PIECES = CHUNKS * 2 * PASSES
 CHUNK_PIECES = 2 * PASSES
 VECTOR_COLS = (192, 192, 192, 128)
+VECTOR_COLS_LO = 32
+VECTOR_COLS_HI = 0
+STAGE = 5
+AHEAD = 8
+ACT_AFTER = (1, 1, 1, 1, 4, 5, 6, 7)
+GROUPS_PER_STEP = 1
+BACKS = 2
+LAG = 2
+BIAS_STEP = 2
 LN_EPS = 1e-5
 LN_COLS = 1024
 
@@ -40,6 +50,7 @@ def tile_crossattentionlayer_pa_kernel(
         keep = ctx.enter_context(tc.tile_pool(name="keep", bufs=1))
         raw_pool = ctx.enter_context(tc.tile_pool(name="raw", bufs=8))
         stage = ctx.enter_context(tc.tile_pool(name="stage", bufs=5))
+        w_stage = ctx.enter_context(tc.tile_pool(name="w_stage", bufs=STAGE))
         w_pool = ctx.enter_context(tc.tile_pool(name="w", bufs=4))
         work = ctx.enter_context(tc.tile_pool(name="work", bufs=2))
         psum_acc = ctx.enter_context(tc.psum_pool(name="psum_acc", bufs=5))
@@ -53,7 +64,7 @@ def tile_crossattentionlayer_pa_kernel(
         c_codes = keep.tile([P, PASSES, TOKENS], U32, align_bytes=64)
         c_scales = keep.tile([P, PASSES, TOKENS], U8, align_bytes=64)
         y_gamma = keep.tile([P, TOKEN_TILES, HID], F32)
-        stats = keep.tile([P, TOKEN_TILES, CHUNKS, 6], F32)
+        stats = keep.tile([P, TOKEN_TILES, CHUNKS + 1, 6], F32)
         gamma_all = const.tile([P, HID], BF16)
 
         ident_f32 = const.tile([P, P], F32)
@@ -97,42 +108,47 @@ def tile_crossattentionlayer_pa_kernel(
         def load_tokens(rows, source, i):
             nc.sync.dma_start(out=rows[:, i, :], in_=source[i])
 
-        for i in range(TOKEN_TILES):
-            load_piece(i)
-            if i == 1:
-                load_tokens(h_rows, hidden_states, 0)
-                load_tokens(h_rows, hidden_states, 1)
-            if i > 1:
-                load_tokens(h_rows, hidden_states, i)
-        for i in range(TOKEN_TILES):
-            load_piece(TOKEN_TILES + i)
-            load_tokens(c_rows, attn_ctx, i)
+        def load_step(n):
+            if n < PIECES:
+                load_piece(n)
+            for t in range(2 * TOKEN_TILES):
+                if ACT_AFTER[t] == n:
+                    m, i = divmod(t, TOKEN_TILES)
+                    load_tokens((h_rows, c_rows)[m], (hidden_states, attn_ctx)[m], i)
+
+        for n in range(AHEAD):
+            load_step(n)
 
         groupeds = {}
         w_mx = {}
 
-        def regroup_piece(n):
-            raw = raws.pop(n)
-            grouped = stage.tile([P, CHUNK, PACK], BF16, align_bytes=64, name="w_grouped")
-            src = raw[:].rearrange("p j (c i) -> p c j i", i=RUN)
+        items = [(n, 0, CHUNK) for n in range(PIECES - PASSES)]
+        for half in range(2):
+            items += [(n, CHUNK // 2 * half, CHUNK // 2 * (half + 1)) for n in range(PIECES - PASSES, PIECES)]
+
+        def regroup_item(s):
+            n, lo, hi = items[s]
+            grouped = w_stage.tile([P, hi - lo, PACK], BF16, align_bytes=64, name="w_grouped")
+            src = raws[n][:, :, lo:hi].rearrange("p j (c i) -> p c j i", i=RUN)
             dst = grouped[:].rearrange("p (c i) j -> p c j i", i=RUN)
-            split = VECTOR_COLS[n // CHUNK_PIECES] // RUN
+            split = (VECTOR_COLS[n // CHUNK_PIECES] if hi - lo == CHUNK else (VECTOR_COLS_LO, VECTOR_COLS_HI)[lo > 0]) // RUN
             nc.scalar.copy(out=dst[:, split:], in_=src[:, split:])
             if split:
                 nc.vector.tensor_copy(out=dst[:, :split], in_=src[:, :split])
-            groupeds[n] = grouped
+            groupeds[s] = grouped
 
-        def quantise_piece(n):
+        def quantise_item(s):
+            n, lo, hi = items[s]
             g = n % PASSES
-            if g == 0:
+            if g == 0 and lo == 0:
                 codes = w_pool.tile([P, PASSES, CHUNK], U32, align_bytes=64, name="w_codes")
                 scales = w_pool.tile([P, PASSES, CHUNK], U8, align_bytes=64, name="w_scales")
                 w_mx[n // PASSES] = (codes, scales)
             codes, scales = w_mx[n // PASSES]
             nc.vector.quantize_mx(
-                out=codes[:, g, :].bitcast(FP8X4),
-                scales=scales[:, g, :],
-                in_=groupeds.pop(n)[:].rearrange("p c j -> p (c j)"),
+                out=codes[:, g, lo:hi].bitcast(FP8X4),
+                scales=scales[:, g, lo:hi],
+                in_=groupeds.pop(s)[:].rearrange("p c j -> p (c j)"),
             )
 
         units = [(m, pair, g) for m in range(2) for pair in range(TOKEN_TILES // 2) for g in range(PASSES)]
@@ -191,11 +207,12 @@ def tile_crossattentionlayer_pa_kernel(
                 one_pass(acc, w_mx[2 * chunk + which], f, x_mx, g)
             accs[which, chunk, f] = acc
 
-        def product_pass(chunk, g):
-            for f in range(FEATURE_TILES):
+        def product_pass(which, chunk, g, features):
+            x_mx = ((h_codes, h_scales), (c_codes, c_scales))[which]
+            for f in features:
                 if g == 0:
-                    accs[1, chunk, f] = psum_acc.tile([P, TOKENS], F32, name="acc")
-                one_pass(accs[1, chunk, f], w_mx[2 * chunk + 1], f, (c_codes, c_scales), g)
+                    accs[which, chunk, f] = psum_acc.tile([P, TOKENS], F32, name="acc")
+                one_pass(accs[which, chunk, f], w_mx[2 * chunk + which], f, x_mx, g)
 
         def sigmoid(chunk, f):
             if f == 0:
@@ -223,88 +240,124 @@ def tile_crossattentionlayer_pa_kernel(
 
         backs = {}
 
-        def back_to_tokens(chunk, i):
-            cols = slice(CHUNK * chunk, CHUNK * (chunk + 1))
-            if chunk == CHUNKS - 1:
-                back = psum_acc.tile([P, CHUNK], F32, name="acc")
-            else:
-                back = psum_t.tile([P, CHUNK], F32, name="t")
-            nc.tensor.matmul(back[:], lhsT=ident_bf16[:], rhs=h_rows[:, i, cols], start=True, stop=False)
-            for f in range(FEATURE_TILES):
+        def columns(chunk, features):
+            return slice(CHUNK * chunk + P * features[0], CHUNK * chunk + P * (features[-1] + 1))
+
+        def back_to_tokens(chunk, features, i, pool=psum_t, name="t"):
+            width = P * len(features)
+            back = pool.tile([P, width], F32, name=name)
+            nc.tensor.matmul(
+                back[:], lhsT=ident_bf16[:], rhs=h_rows[:, i, columns(chunk, features)], start=True, stop=False
+            )
+            for f in features:
+                place = P * (f - features[0])
                 nc.tensor.matmul(
-                    back[:, P * f : P * (f + 1)],
+                    back[:, place : place + P],
                     lhsT=gates[chunk][:, f, P * i : P * (i + 1)],
                     rhs=ident_f32[:],
                     is_transpose=True,
                     start=False,
-                    stop=(f == FEATURE_TILES - 1),
+                    stop=(f == features[-1]),
                 )
-            backs[chunk, i] = back
+            backs[chunk, features[0], i] = back
 
-        def take_stats(chunk, i):
-            nc.vector.bn_stats(out=stats[:, i, chunk, :], in_=backs[chunk, i][:])
+        def take_stats(chunk, features, i):
+            nc.vector.bn_stats(out=stats[:, i, chunk + (features[0] > 0), :], in_=backs[chunk, features[0], i][:])
 
-        def take_y(chunk, i):
-            cols = slice(CHUNK * chunk, CHUNK * (chunk + 1))
-            nc.vector.tensor_tensor(out=y_gamma[:, i, cols], in0=backs.pop((chunk, i))[:], in1=gamma_all[:, cols], op=ALU.mult)
+        def take_y(chunk, features, i):
+            cols = columns(chunk, features)
+            nc.vector.tensor_tensor(
+                out=y_gamma[:, i, cols], in0=backs.pop((chunk, features[0], i))[:], in1=gamma_all[:, cols], op=ALU.mult
+            )
 
         last = CHUNKS - 1
-        for s in range(PIECES + 1):
-            if s == 1:
-                nc.sync.dma_start(out=gamma_all[:], in_=ln_gamma.partition_broadcast(P))
+        due_s = {}
+        due_v = {}
+        due_pe = {}
+        unit_jobs = {}
+        for pair in range(TOKEN_TILES):
+            unit_jobs[ACT_AFTER[2 * pair + 1] + 1] = unit_jobs.get(ACT_AFTER[2 * pair + 1] + 1, []) + list(range(PASSES * pair, PASSES * (pair + 1)))
+        ALL, LOW, HIGH = range(FEATURE_TILES), range(FEATURE_TILES // 2), range(FEATURE_TILES // 2, FEATURE_TILES)
+        products = []
+        for chunk in range(CHUNKS):
+            for which in range(2):
+                final = (which, chunk) == (1, last)
+                features = LOW if final else ALL
+                for f in features:
+                    first = CHUNK_PIECES * chunk + PASSES * (which + 1) - 1 + (1 if final else LAG)
+                    if chunk > 0 or which == 1:
+                        products.append((which, chunk, features, f, max(first, ACT_AFTER[TOKEN_TILES * (which + 1) - 1] + 1)))
+        for s in range(len(items) + 1):
+            if s == BIAS_STEP:
+                make_bias_cols()
                 nc.sync.dma_start(out=norm_rows[0:1, :], in_=ln_gamma.unsqueeze(0))
                 nc.sync.dma_start(out=norm_rows[1:2, :], in_=ln_gamma.unsqueeze(0))
                 nc.sync.dma_start(out=norm_rows[2:3, :], in_=ln_beta.unsqueeze(0))
-                make_bias_cols()
-            for chunk in range(CHUNKS):
-                t = s - CHUNK_PIECES * chunk
-                if 6 <= t < 10:
-                    sigmoid(chunk, t - 6)
-                if 10 <= t < 14 and chunk != last:
-                    apply_gate(chunk, t - 10)
-                if 15 <= t < 17:
-                    for i in (2 * (t - 15), 2 * (t - 15) + 1):
-                        take_stats(chunk, i)
-                        take_y(chunk, i)
-            if s < PIECES:
-                regroup_piece(s)
-            ahead = s + 2 * TOKEN_TILES
-            if ahead < PIECES:
-                load_piece(ahead)
+            if s == 9:
+                nc.sync.dma_start(out=gamma_all[:], in_=ln_gamma.partition_broadcast(P))
+            for job in due_s.pop(s, ()):
+                job()
+            now = unit_jobs.get(s, [])
+            for i in range(0, len(now), 2):
+                flip_unit(now[i])
+                flip_unit(now[i + 1])
+                group_unit(now[i])
+                group_unit(now[i + 1])
+                if i:
+                    quantise_unit(now[i - 2])
+                    quantise_unit(now[i - 1])
+            if s < len(items):
+                regroup_item(s)
+            for k in now[-2:]:
+                quantise_unit(k)
+            load_step(s + AHEAD)
             if s >= 1:
-                quantise_piece(s - 1)
-            first = 2 * (s - 2)
-            if s % 2 == 0 and 0 <= first < len(units):
-                for k in (first, first + 2):
-                    flip_unit(k)
-                    flip_unit(k + 1)
-                    group_unit(k)
-                    group_unit(k + 1)
-            first = 2 * (s - 3)
-            if s % 2 == 1 and 0 <= first < len(units):
-                for k in range(first, first + PASSES):
-                    quantise_unit(k)
-            for chunk in range(CHUNKS):
-                t = s - CHUNK_PIECES * chunk
-                if 5 <= t < 9:
-                    product(0, chunk, t - 5)
-                if 9 <= t < 13 and chunk != last:
-                    product(1, chunk, t - 9)
-                if chunk == last and 5 <= t:
-                    product_pass(chunk, t - 5)
-                if 14 <= t < 16:
-                    for i in (2 * (t - 14), 2 * (t - 14) + 1):
-                        back_to_tokens(chunk, i)
+                quantise_item(s - 1)
+            for job in due_v.pop(s, ()):
+                job()
+            start = ACT_AFTER[TOKEN_TILES - 1] + 1
+            if s == start:
+                for g in range(s):
+                    if g < PASSES:
+                        product_pass(0, 0, g, ALL)
+            elif start < s <= PASSES:
+                product_pass(0, 0, s - 1, ALL)
+            if s == max(start, PASSES):
+                for f in ALL:
+                    due_s.setdefault(s + 1, []).append(partial(sigmoid, 0, f))
+            g = s - 1 - (len(items) - PASSES)
+            if g >= 0:
+                product_pass(1, last, g, HIGH)
+            for turn in range(2 if s > PIECES - PASSES else GROUPS_PER_STEP):
+                if products and products[0][4] <= s:
+                    which, chunk, features, f, first = products.pop(0)
+                    product(which, chunk, f)
+                    if which == 0:
+                        due_s.setdefault(s + 1, []).append(partial(sigmoid, chunk, f))
+                    else:
+                        due_v.setdefault(s + 1, []).append(partial(apply_gate, chunk, f))
+                        if f == features[-1]:
+                            for i in range(TOKEN_TILES):
+                                t = s + (1 if features is LOW else 2) + i // BACKS
+                                due_pe.setdefault(t, []).append(partial(back_to_tokens, chunk, features, i))
+                                due_v.setdefault(t + 1, []).append(partial(take_stats, chunk, features, i))
+                                due_v.setdefault(t + 1, []).append(partial(take_y, chunk, features, i))
+            for job in due_pe.pop(s, ()):
+                job()
+        for due in (due_s, due_pe, due_v):
+            for s in sorted(due):
+                for job in due[s]:
+                    job()
+        assert not products
 
-        sigmoid(last, 3)
         sqrt_warm = const.tile([P, 1], F32)
         nc.scalar.sqrt(out=sqrt_warm[:], in_=gates[last][:, 3, 0:1])
-        for f in range(FEATURE_TILES):
+        for f in HIGH:
             apply_gate(last, f)
         for i in range(TOKEN_TILES):
-            back_to_tokens(last, i)
+            back_to_tokens(last, HIGH, i, psum_acc, "acc")
         for i in range(TOKEN_TILES):
-            take_stats(last, i)
+            take_stats(last, HIGH, i)
 
         mean_var = keep.tile([P, TOKEN_TILES, 2], F32)
         for i in range(TOKEN_TILES):
@@ -312,16 +365,18 @@ def tile_crossattentionlayer_pa_kernel(
         rstd = keep.tile([P, TOKEN_TILES], F32)
         nc.vector.tensor_scalar(out=rstd[:], in0=mean_var[:, :, 1], scalar1=LN_EPS, scalar2=None, op0=ALU.add)
         nc.scalar.sqrt(out=rstd[:], in_=rstd[:])
-        take_y(last, 0)
+        take_y(last, HIGH, 0)
         nc.vector.reciprocal(out=rstd[:], in_=rstd[:])
         shift = keep.tile([P, TOKEN_TILES], F32)
         nc.vector.scalar_tensor_tensor(
             out=shift[:], in0=mean_var[:, :, 0], scalar=-1.0, in1=rstd[:], op0=ALU.mult, op1=ALU.mult
         )
-        nc.vector.tensor_copy(out=shift_cols[:, :, 0], in_=shift[:])
+        nc.vector.scalar_tensor_tensor(
+            out=shift_cols[:, :, 0], in0=mean_var[:, :, 0], scalar=-1.0, in1=rstd[:], op0=ALU.mult, op1=ALU.mult
+        )
         nc.vector.tensor_tensor(out=shift_cols[:, :, 1], in0=shift[:], in1=shift_cols[:, :, 0], op=ALU.subtract)
         for i in range(1, TOKEN_TILES):
-            take_y(last, i)
+            take_y(last, HIGH, i)
         shift_t = psum_t.tile([P, TOKENS], BF16, name="t")
         for i in range(TOKEN_TILES):
             nc.tensor.transpose(shift_t[:, P * i : P * (i + 1)], shift_cols[:, i, :], ident_bf16[:])

@@ -26,7 +26,7 @@ RUN = 4
 PIECES = CHUNKS * 2 * PASSES
 CHUNK_PIECES = 2 * PASSES
 VECTOR_COLS = (192, 192, 192, 128)
-VECTOR_COLS_LO = 32
+VECTOR_COLS_LO = 0
 VECTOR_COLS_HI = 0
 STAGE = 5
 AHEAD = 8
@@ -35,6 +35,7 @@ GROUPS_PER_STEP = 1
 BACKS = 2
 LAG = 2
 BIAS_STEP = 2
+LOW_LAG = 2
 LN_EPS = 1e-5
 LN_COLS = 1024
 
@@ -53,8 +54,8 @@ def tile_crossattentionlayer_pa_kernel(
         w_stage = ctx.enter_context(tc.tile_pool(name="w_stage", bufs=STAGE))
         w_pool = ctx.enter_context(tc.tile_pool(name="w", bufs=4))
         work = ctx.enter_context(tc.tile_pool(name="work", bufs=2))
-        psum_acc = ctx.enter_context(tc.psum_pool(name="psum_acc", bufs=5))
-        psum_t = ctx.enter_context(tc.psum_pool(name="psum_t", bufs=3))
+        psum_acc = ctx.enter_context(tc.psum_pool(name="psum_acc", bufs=4))
+        psum_t = ctx.enter_context(tc.psum_pool(name="psum_t", bufs=4))
         ctx.enter_context(tc.manual_schedule())
 
         h_rows = keep.tile([P, TOKEN_TILES, HID], BF16)
@@ -83,6 +84,8 @@ def tile_crossattentionlayer_pa_kernel(
         nc.vector.memset(shift_cols[:], 0.0)
         nc.vector.memset(shift_cols[:, :, 2:3], 1.0)
         bias_cols = const.tile([P, 2 * n_tiles], F32)
+        eps_col = const.tile([P, 1], F32)
+        nc.vector.memset(eps_col[:], LN_EPS)
 
         def make_bias_cols():
             bias_t = psum_t.tile([P, P], BF16, name="t")
@@ -226,48 +229,55 @@ def tile_crossattentionlayer_pa_kernel(
                 scale=1.0,
             )
 
-        def apply_gate(chunk, f):
+        def apply_gate(chunk, f, tokens=slice(0, TOKENS)):
             bo_col = FEATURE_TILES * chunk + f
             gate = gates[chunk]
             nc.vector.scalar_tensor_tensor(
-                out=gate[:, f, :],
-                in0=accs.pop((1, chunk, f))[:],
+                out=gate[:, f, tokens],
+                in0=accs[1, chunk, f][:, tokens],
                 scalar=bias_cols[:, bo_col : bo_col + 1],
-                in1=gate[:, f, :],
+                in1=gate[:, f, tokens],
                 op0=ALU.add,
                 op1=ALU.mult,
             )
 
         backs = {}
+        ALL, LOW, HIGH = range(FEATURE_TILES), range(FEATURE_TILES // 2), range(FEATURE_TILES // 2, FEATURE_TILES)
 
         def columns(chunk, features):
             return slice(CHUNK * chunk + P * features[0], CHUNK * chunk + P * (features[-1] + 1))
 
-        def back_to_tokens(chunk, features, i, pool=psum_t, name="t"):
-            width = P * len(features)
-            back = pool.tile([P, width], F32, name=name)
+        def back_to_tokens(chunk, features, i):
+            if features[0] == 0:
+                backs[chunk, i] = psum_t.tile([P, CHUNK], F32, name="t")
+            back = backs[chunk, i]
             nc.tensor.matmul(
-                back[:], lhsT=ident_bf16[:], rhs=h_rows[:, i, columns(chunk, features)], start=True, stop=False
+                back[:, P * features[0] : P * (features[-1] + 1)],
+                lhsT=ident_bf16[:],
+                rhs=h_rows[:, i, columns(chunk, features)],
+                start=True,
+                stop=False,
             )
             for f in features:
-                place = P * (f - features[0])
                 nc.tensor.matmul(
-                    back[:, place : place + P],
+                    back[:, P * f : P * (f + 1)],
                     lhsT=gates[chunk][:, f, P * i : P * (i + 1)],
                     rhs=ident_f32[:],
                     is_transpose=True,
                     start=False,
                     stop=(f == features[-1]),
                 )
-            backs[chunk, features[0], i] = back
 
         def take_stats(chunk, features, i):
-            nc.vector.bn_stats(out=stats[:, i, chunk + (features[0] > 0), :], in_=backs[chunk, features[0], i][:])
+            nc.vector.bn_stats(
+                out=stats[:, i, chunk + (features[0] > 0), :],
+                in_=backs[chunk, i][:, P * features[0] : P * (features[-1] + 1)],
+            )
 
-        def take_y(chunk, features, i):
-            cols = columns(chunk, features)
+        def take_y(chunk, i):
+            cols = columns(chunk, ALL)
             nc.vector.tensor_tensor(
-                out=y_gamma[:, i, cols], in0=backs.pop((chunk, features[0], i))[:], in1=gamma_all[:, cols], op=ALU.mult
+                out=y_gamma[:, i, cols], in0=backs.pop((chunk, i))[:], in1=gamma_all[:, cols], op=ALU.mult
             )
 
         last = CHUNKS - 1
@@ -277,7 +287,6 @@ def tile_crossattentionlayer_pa_kernel(
         unit_jobs = {}
         for pair in range(TOKEN_TILES):
             unit_jobs[ACT_AFTER[2 * pair + 1] + 1] = unit_jobs.get(ACT_AFTER[2 * pair + 1] + 1, []) + list(range(PASSES * pair, PASSES * (pair + 1)))
-        ALL, LOW, HIGH = range(FEATURE_TILES), range(FEATURE_TILES // 2), range(FEATURE_TILES // 2, FEATURE_TILES)
         products = []
         for chunk in range(CHUNKS):
             for which in range(2):
@@ -340,8 +349,11 @@ def tile_crossattentionlayer_pa_kernel(
                             for i in range(TOKEN_TILES):
                                 t = s + (1 if features is LOW else 2) + i // BACKS
                                 due_pe.setdefault(t, []).append(partial(back_to_tokens, chunk, features, i))
-                                due_v.setdefault(t + 1, []).append(partial(take_stats, chunk, features, i))
-                                due_v.setdefault(t + 1, []).append(partial(take_y, chunk, features, i))
+                                if features is LOW:
+                                    due_v.setdefault(t + LOW_LAG, []).append(partial(take_stats, chunk, features, i))
+                                else:
+                                    due_v.setdefault(t + 1, []).append(partial(take_stats, chunk, features, i))
+                                    due_v.setdefault(t + 1, []).append(partial(take_y, chunk, i))
             for job in due_pe.pop(s, ()):
                 job()
         for due in (due_s, due_pe, due_v):
@@ -350,41 +362,66 @@ def tile_crossattentionlayer_pa_kernel(
                     job()
         assert not products
 
-        sqrt_warm = const.tile([P, 1], F32)
-        nc.scalar.sqrt(out=sqrt_warm[:], in_=gates[last][:, 3, 0:1])
-        for f in HIGH:
-            apply_gate(last, f)
+        rstd = keep.tile([P, TOKEN_TILES], F32)
+        nc.scalar.activation(
+            out=rstd[:, 0:1], in_=gates[last][:, 3, 0:1], func=ACT.Abs_reciprocal_sqrt, bias=eps_col[:], scale=1.0
+        )
+        pairs = [(0, 1), (2, 3)]
+        for pair in pairs:
+            for f in HIGH:
+                apply_gate(last, f, slice(P * pair[0], P * (pair[-1] + 1)))
         for i in range(TOKEN_TILES):
-            back_to_tokens(last, HIGH, i, psum_acc, "acc")
-        for i in range(TOKEN_TILES):
-            take_stats(last, HIGH, i)
+            back_to_tokens(last, HIGH, i)
 
         mean_var = keep.tile([P, TOKEN_TILES, 2], F32)
-        for i in range(TOKEN_TILES):
-            nc.vector.bn_aggr(out=mean_var[:, i, :], in_=stats[:, i, :, :].rearrange("p c s -> p (c s)"))
-        rstd = keep.tile([P, TOKEN_TILES], F32)
-        nc.vector.tensor_scalar(out=rstd[:], in0=mean_var[:, :, 1], scalar1=LN_EPS, scalar2=None, op0=ALU.add)
-        nc.scalar.sqrt(out=rstd[:], in_=rstd[:])
-        take_y(last, HIGH, 0)
-        nc.vector.reciprocal(out=rstd[:], in_=rstd[:])
         shift = keep.tile([P, TOKEN_TILES], F32)
-        nc.vector.scalar_tensor_tensor(
-            out=shift[:], in0=mean_var[:, :, 0], scalar=-1.0, in1=rstd[:], op0=ALU.mult, op1=ALU.mult
-        )
-        nc.vector.scalar_tensor_tensor(
-            out=shift_cols[:, :, 0], in0=mean_var[:, :, 0], scalar=-1.0, in1=rstd[:], op0=ALU.mult, op1=ALU.mult
-        )
-        nc.vector.tensor_tensor(out=shift_cols[:, :, 1], in0=shift[:], in1=shift_cols[:, :, 0], op=ALU.subtract)
-        for i in range(1, TOKEN_TILES):
-            take_y(last, HIGH, i)
-        shift_t = psum_t.tile([P, TOKENS], BF16, name="t")
-        for i in range(TOKEN_TILES):
-            nc.tensor.transpose(shift_t[:, P * i : P * (i + 1)], shift_cols[:, i, :], ident_bf16[:])
         shift_rows = keep.tile([P, TOKENS], BF16)
-        nc.scalar.copy(out=shift_rows[:], in_=shift_t[:])
+
+        def aggregate(pair):
+            for i in pair:
+                take_stats(last, HIGH, i)
+            for i in pair:
+                nc.vector.bn_aggr(out=mean_var[:, i, :], in_=stats[:, i, :, :].rearrange("p c s -> p (c s)"))
+            both = slice(pair[0], pair[-1] + 1)
+            nc.scalar.activation(
+                out=rstd[:, both], in_=mean_var[:, both, 1], func=ACT.Abs_reciprocal_sqrt, bias=eps_col[:], scale=1.0
+            )
+
+        def split_shift(pair):
+            both = slice(pair[0], pair[-1] + 1)
+            for out_ap in (shift_cols[:, both, 0], shift[:, both]):
+                nc.vector.scalar_tensor_tensor(
+                    out=out_ap, in0=mean_var[:, both, 0], scalar=-1.0, in1=rstd[:, both], op0=ALU.mult, op1=ALU.mult
+                )
+
+        def split_shift_low(pair):
+            both = slice(pair[0], pair[-1] + 1)
+            nc.vector.tensor_tensor(
+                out=shift_cols[:, both, 1], in0=shift[:, both], in1=shift_cols[:, both, 0], op=ALU.subtract
+            )
+
+        def shift_to_rows(pair):
+            flat = psum_acc.tile([P, 2 * P], BF16, name="acc")
+            for i in pair:
+                nc.tensor.transpose(flat[:, P * (i - pair[0]) : P * (i - pair[0] + 1)], shift_cols[:, i, :], ident_bf16[:])
+            nc.scalar.copy(out=shift_rows[:, P * pair[0] : P * (pair[-1] + 1)], in_=flat[:])
+
+        aggregate(pairs[0])
+        take_y(last, 0)
+        split_shift(pairs[0])
+        aggregate(pairs[1])
+        split_shift_low(pairs[0])
+        shift_to_rows(pairs[0])
+        take_y(last, 1)
+        split_shift(pairs[1])
+        split_shift_low(pairs[1])
 
         out_rows = out.rearrange("b s d -> s b d")
         for i in range(TOKEN_TILES):
+            if i == 1:
+                shift_to_rows(pairs[1])
+            if i in pairs[1]:
+                take_y(last, i)
             for c in range(CHUNKS):
                 cols = slice(CHUNK * c, CHUNK * (c + 1))
                 offset = psum_acc.tile([P, CHUNK], F32, name="acc")
@@ -399,6 +436,8 @@ def tile_crossattentionlayer_pa_kernel(
                     op0=ALU.mult,
                     op1=ALU.add,
                 )
-                if (c + 1) * CHUNK % LN_COLS == 0:
+                if i == TOKEN_TILES - 1 and c >= CHUNKS // 2:
+                    nc.sync.dma_start(out=out_rows[:, i, cols], in_=y_gamma[:, i, cols])
+                elif (c + 1) * CHUNK % LN_COLS == 0:
                     cols = slice((c + 1) * CHUNK - LN_COLS, (c + 1) * CHUNK)
                     nc.sync.dma_start(out=out_rows[:, i, cols], in_=y_gamma[:, i, cols])

@@ -103,9 +103,11 @@ def tile_crossattentionlayer_pa_kernel(
             which, g, cols = piece_of(n)
             raw = raw_pool.tile([P, PACK, CHUNK], BF16, name="raw")
             w = (Wg, Wo)[which]
-            nc.sync.dma_start(
-                out=raw[:], in_=w[K_PASS * g : K_PASS * (g + 1), cols].rearrange("(p j) c -> p j c", j=PACK)
-            )
+            for u in range(2):
+                rows = slice(K_PASS * g + 2 * P * u, K_PASS * g + 2 * P * (u + 1))
+                nc.sync.dma_start(
+                    out=raw[:, 2 * u : 2 * u + 2, :], in_=w[rows, cols].rearrange("(p e) c -> p e c", e=2)
+                )
             raws[n] = raw
 
         def load_tokens(rows, source, i):
@@ -166,7 +168,9 @@ def tile_crossattentionlayer_pa_kernel(
                 for s in range(2):
                     words = rows[:, 2 * pair + s, :].bitcast(F32)
                     nc.tensor.transpose(
-                        flipped[:, u, P * s : P * (s + 1)], words[:, 2 * P * g + u : 2 * P * (g + 1) : 2], ident_f32[:]
+                        flipped[:, u, P * s : P * (s + 1)],
+                        words[:, 2 * P * g + P * u : 2 * P * g + P * (u + 1)],
+                        ident_f32[:],
                     )
             flips[k] = flipped
 

@@ -25,9 +25,7 @@ FEATURE_TILES = CHUNK // P
 RUN = 4
 PIECES = CHUNKS * 2 * PASSES
 CHUNK_PIECES = 2 * PASSES
-VECTOR_COLS = (192, 192, 192, 128)
-VECTOR_COLS_LO = 0
-VECTOR_COLS_HI = 0
+VECTOR_COLS = ((0, 384), (0, 384), (0, 320), (0, 256))
 STAGE = 5
 AHEAD = 8
 ACT_AFTER = (1, 1, 1, 1, 4, 5, 6, 7)
@@ -36,6 +34,8 @@ BACKS = 2
 LAG = 2
 BIAS_STEP = 2
 LOW_LAG = 2
+SCALAR_FROM = 2
+ORDER = (1, 0, 2, 3)
 LN_EPS = 1e-5
 LN_COLS = 1024
 
@@ -136,7 +136,7 @@ def tile_crossattentionlayer_pa_kernel(
             grouped = w_stage.tile([P, hi - lo, PACK], BF16, align_bytes=64, name="w_grouped")
             src = raws[n][:, :, lo:hi].rearrange("p j (c i) -> p c j i", i=RUN)
             dst = grouped[:].rearrange("p (c i) j -> p c j i", i=RUN)
-            split = (VECTOR_COLS[n // CHUNK_PIECES] if hi - lo == CHUNK else (VECTOR_COLS_LO, VECTOR_COLS_HI)[lo > 0]) // RUN
+            split = (VECTOR_COLS[n // CHUNK_PIECES][n % 2] if hi - lo == CHUNK else 0) // RUN
             nc.scalar.copy(out=dst[:, split:], in_=src[:, split:])
             if split:
                 nc.vector.tensor_copy(out=dst[:, :split], in_=src[:, :split])
@@ -420,28 +420,43 @@ def tile_crossattentionlayer_pa_kernel(
         split_shift(pairs[1])
         split_shift_low(pairs[1])
 
+        def shift_and_beta(bank, i, cols, start):
+            nc.tensor.matmul(
+                bank[:], lhsT=shift_rows[:, P * i : P * (i + 1)], rhs=norm_rows[:, cols], start=start, stop=True
+            )
+
         out_rows = out.rearrange("b s d -> s b d")
         for i in range(TOKEN_TILES):
             if i == 1:
                 shift_to_rows(pairs[1])
             if i in pairs[1]:
                 take_y(last, i)
-            for c in range(CHUNKS):
+            on_scalar = (0,) if i >= SCALAR_FROM else ()
+            if on_scalar:
+                diagonal = work.tile([P, P], F32)
+                nc.scalar.activation(out=diagonal[:], in_=ident_f32[:], func=ACT.Copy, scale=rstd[:, i : i + 1])
+            for c in (ORDER if on_scalar else range(CHUNKS)):
                 cols = slice(CHUNK * c, CHUNK * (c + 1))
-                offset = psum_acc.tile([P, CHUNK], F32, name="acc")
-                nc.tensor.matmul(
-                    offset[:], lhsT=shift_rows[:, P * i : P * (i + 1)], rhs=norm_rows[:, cols], start=True, stop=True
-                )
-                nc.vector.scalar_tensor_tensor(
-                    out=y_gamma[:, i, cols],
-                    in0=y_gamma[:, i, cols],
-                    scalar=rstd[:, i : i + 1],
-                    in1=offset[:],
-                    op0=ALU.mult,
-                    op1=ALU.add,
-                )
-                if i == TOKEN_TILES - 1 and c >= CHUNKS // 2:
+                bank = psum_acc.tile([P, CHUNK], F32, name="acc")
+                if c in on_scalar:
+                    nc.tensor.matmul(bank[:], lhsT=diagonal[:], rhs=y_gamma[:, i, cols], start=True, stop=False)
+                    shift_and_beta(bank, i, cols, False)
+                    nc.scalar.copy(out=y_gamma[:, i, cols], in_=bank[:])
+                else:
+                    shift_and_beta(bank, i, cols, True)
+                    nc.vector.scalar_tensor_tensor(
+                        out=y_gamma[:, i, cols],
+                        in0=y_gamma[:, i, cols],
+                        scalar=rstd[:, i : i + 1],
+                        in1=bank[:],
+                        op0=ALU.mult,
+                        op1=ALU.add,
+                    )
+                small = (i == 0 and c < CHUNKS // 2) or (i == TOKEN_TILES - 1 and c >= CHUNKS // 2)
+                if small:
                     nc.sync.dma_start(out=out_rows[:, i, cols], in_=y_gamma[:, i, cols])
-                elif (c + 1) * CHUNK % LN_COLS == 0:
-                    cols = slice((c + 1) * CHUNK - LN_COLS, (c + 1) * CHUNK)
+                elif on_scalar and c == 0:
+                    nc.sync.dma_start(out=out_rows[:, i, 0:LN_COLS], in_=y_gamma[:, i, 0:LN_COLS])
+                elif c % 2 == 1 and not (on_scalar and c == 1):
+                    cols = slice((c - 1) * CHUNK, (c + 1) * CHUNK)
                     nc.sync.dma_start(out=out_rows[:, i, cols], in_=y_gamma[:, i, cols])

@@ -34,8 +34,6 @@ BACKS = 2
 LAG = 2
 BIAS_STEP = 2
 LOW_LAG = 2
-SCALAR_FROM = 2
-ORDER = (1, 0, 2, 3)
 LN_EPS = 1e-5
 LN_COLS = 1024
 
@@ -420,43 +418,28 @@ def tile_crossattentionlayer_pa_kernel(
         split_shift(pairs[1])
         split_shift_low(pairs[1])
 
-        def shift_and_beta(bank, i, cols, start):
-            nc.tensor.matmul(
-                bank[:], lhsT=shift_rows[:, P * i : P * (i + 1)], rhs=norm_rows[:, cols], start=start, stop=True
-            )
-
         out_rows = out.rearrange("b s d -> s b d")
         for i in range(TOKEN_TILES):
             if i == 1:
                 shift_to_rows(pairs[1])
             if i in pairs[1]:
                 take_y(last, i)
-            on_scalar = (0,) if i >= SCALAR_FROM else ()
-            if on_scalar:
-                diagonal = work.tile([P, P], F32)
-                nc.scalar.activation(out=diagonal[:], in_=ident_f32[:], func=ACT.Copy, scale=rstd[:, i : i + 1])
-            for c in (ORDER if on_scalar else range(CHUNKS)):
+            for c in range(CHUNKS):
                 cols = slice(CHUNK * c, CHUNK * (c + 1))
-                bank = psum_acc.tile([P, CHUNK], F32, name="acc")
-                if c in on_scalar:
-                    nc.tensor.matmul(bank[:], lhsT=diagonal[:], rhs=y_gamma[:, i, cols], start=True, stop=False)
-                    shift_and_beta(bank, i, cols, False)
-                    nc.scalar.copy(out=y_gamma[:, i, cols], in_=bank[:])
-                else:
-                    shift_and_beta(bank, i, cols, True)
-                    nc.vector.scalar_tensor_tensor(
-                        out=y_gamma[:, i, cols],
-                        in0=y_gamma[:, i, cols],
-                        scalar=rstd[:, i : i + 1],
-                        in1=bank[:],
-                        op0=ALU.mult,
-                        op1=ALU.add,
-                    )
-                small = (i == 0 and c < CHUNKS // 2) or (i == TOKEN_TILES - 1 and c >= CHUNKS // 2)
-                if small:
+                offset = psum_acc.tile([P, CHUNK], F32, name="acc")
+                nc.tensor.matmul(
+                    offset[:], lhsT=shift_rows[:, P * i : P * (i + 1)], rhs=norm_rows[:, cols], start=True, stop=True
+                )
+                nc.vector.scalar_tensor_tensor(
+                    out=y_gamma[:, i, cols],
+                    in0=y_gamma[:, i, cols],
+                    scalar=rstd[:, i : i + 1],
+                    in1=offset[:],
+                    op0=ALU.mult,
+                    op1=ALU.add,
+                )
+                if (i == 0 and c < CHUNKS // 2) or (i == TOKEN_TILES - 1 and c >= CHUNKS // 2):
                     nc.sync.dma_start(out=out_rows[:, i, cols], in_=y_gamma[:, i, cols])
-                elif on_scalar and c == 0:
-                    nc.sync.dma_start(out=out_rows[:, i, 0:LN_COLS], in_=y_gamma[:, i, 0:LN_COLS])
-                elif c % 2 == 1 and not (on_scalar and c == 1):
-                    cols = slice((c - 1) * CHUNK, (c + 1) * CHUNK)
+                elif (c + 1) * CHUNK % LN_COLS == 0:
+                    cols = slice((c + 1) * CHUNK - LN_COLS, (c + 1) * CHUNK)
                     nc.sync.dma_start(out=out_rows[:, i, cols], in_=y_gamma[:, i, cols])

@@ -54,7 +54,6 @@ def tile_crossattentionlayer_pa_kernel(
         work = ctx.enter_context(tc.tile_pool(name="work", bufs=2))
         psum_acc = ctx.enter_context(tc.psum_pool(name="psum_acc", bufs=4))
         psum_t = ctx.enter_context(tc.psum_pool(name="psum_t", bufs=4))
-        ctx.enter_context(tc.manual_schedule())
 
         h_rows = keep.tile([P, TOKEN_TILES, HID], BF16)
         c_rows = keep.tile([P, TOKEN_TILES, HID], BF16)

from contextlib import ExitStack
from functools import partial

import concourse.mybir as mybir
from concourse.masks import make_identity

F32 = mybir.dt.float32
BF16 = mybir.dt.bfloat16
U32 = mybir.dt.uint32
U8 = mybir.dt.uint8
FP8X4 = mybir.dt.float8_e4m3fn_x4
ALU = mybir.AluOpType
ACT = mybir.ActivationFunctionType

P = 128
PACK = 4
K_PASS = P * PACK
HID = 2048
PASSES = HID // K_PASS
TOKEN_TILES = 4
TOKENS = TOKEN_TILES * P
CHUNK = 512
CHUNKS = HID // CHUNK
FEATURE_TILES = CHUNK // P
RUN = 4
PIECES = CHUNKS * 2 * PASSES
CHUNK_PIECES = 2 * PASSES
VECTOR_COLS = ((0, 384), (0, 384), (0, 320), (0, 256))
STAGE = 5
AHEAD = 8
ACT_AFTER = (1, 1, 1, 1, 4, 5, 6, 7)
GROUPS_PER_STEP = 1
BACKS = 2
LAG = 2
BIAS_STEP = 2
LOW_LAG = 2
LN_EPS = 1e-5
LN_COLS = 1024

FLOPS = 2 * 2 * TOKENS * HID * HID


def tile_crossattentionlayer_pa_kernel(
    tc, hidden_states, attn_ctx, Wo, bo, Wg, bg, ln_gamma, ln_beta, out
):
    nc = tc.nc
    with ExitStack() as ctx:
        const = ctx.enter_context(tc.tile_pool(name="const", bufs=1))
        keep = ctx.enter_context(tc.tile_pool(name="keep", bufs=1))
        raw_pool = ctx.enter_context(tc.tile_pool(name="raw", bufs=8))
        stage = ctx.enter_context(tc.tile_pool(name="stage", bufs=5))
        w_stage = ctx.enter_context(tc.tile_pool(name="w_stage", bufs=STAGE))
        w_pool = ctx.enter_context(tc.tile_pool(name="w", bufs=4))
        work = ctx.enter_context(tc.tile_pool(name="work", bufs=2))
        psum_acc = ctx.enter_context(tc.psum_pool(name="psum_acc", bufs=4))
        psum_t = ctx.enter_context(tc.psum_pool(name="psum_t", bufs=4))

        h_rows = keep.tile([P, TOKEN_TILES, HID], BF16)
        c_rows = keep.tile([P, TOKEN_TILES, HID], BF16)
        h_codes = keep.tile([P, PASSES, TOKENS], U32, align_bytes=64)
        h_scales = keep.tile([P, PASSES, TOKENS], U8, align_bytes=64)
        c_codes = keep.tile([P, PASSES, TOKENS], U32, align_bytes=64)
        c_scales = keep.tile([P, PASSES, TOKENS], U8, align_bytes=64)
        y_gamma = keep.tile([P, TOKEN_TILES, HID], F32)
        stats = keep.tile([P, TOKEN_TILES, CHUNKS + 1, 6], F32)
        gamma_all = const.tile([P, HID], BF16)

        ident_f32 = const.tile([P, P], F32)
        make_identity(nc, ident_f32[:])
        ident_bf16 = const.tile([P, P], BF16)
        make_identity(nc, ident_bf16[:])
        norm_rows = const.tile([P, HID], BF16)
        nc.gpsimd.memset(norm_rows[:], 0.0)

        n_tiles = HID // P
        bias_rows = const.tile([P, P], BF16)
        nc.vector.memset(bias_rows[:], 0.0)
        nc.scalar.dma_start(out=bias_rows[0:n_tiles, :], in_=bo.rearrange("(c p) -> c p", p=P))
        nc.scalar.dma_start(out=bias_rows[n_tiles : 2 * n_tiles, :], in_=bg.rearrange("(c p) -> c p", p=P))
        shift_cols = const.tile([P, TOKEN_TILES, P], BF16)
        nc.vector.memset(shift_cols[:], 0.0)
        nc.vector.memset(shift_cols[:, :, 2:3], 1.0)
        bias_cols = const.tile([P, 2 * n_tiles], F32)
        eps_col = const.tile([P, 1], F32)
        nc.vector.memset(eps_col[:], LN_EPS)

        def make_bias_cols():
            bias_t = psum_t.tile([P, P], BF16, name="t")
            nc.tensor.transpose(bias_t[:], bias_rows[:], ident_bf16[:])
            nc.vector.tensor_copy(out=bias_cols[:], in_=bias_t[:, 0 : 2 * n_tiles])

        def piece_of(n):
            chunk, rest = divmod(n, CHUNK_PIECES)
            which, g = divmod(rest, PASSES)
            return which, g, slice(CHUNK * chunk, CHUNK * (chunk + 1))

        raws = {}

        def load_piece(n):
            which, g, cols = piece_of(n)
            raw = raw_pool.tile([P, PACK, CHUNK], BF16, name="raw")
            w = (Wg, Wo)[which]
            for u in range(2):
                rows = slice(K_PASS * g + 2 * P * u, K_PASS * g + 2 * P * (u + 1))
                nc.sync.dma_start(
                    out=raw[:, 2 * u : 2 * u + 2, :], in_=w[rows, cols].rearrange("(p e) c -> p e c", e=2)
                )
            raws[n] = raw

        def load_tokens(rows, source, i):
            nc.sync.dma_start(out=rows[:, i, :], in_=source[i])

        def load_step(n):
            if n < PIECES:
                load_piece(n)
            for t in range(2 * TOKEN_TILES):
                if ACT_AFTER[t] == n:
                    m, i = divmod(t, TOKEN_TILES)
                    load_tokens((h_rows, c_rows)[m], (hidden_states, attn_ctx)[m], i)

        for n in range(AHEAD):
            load_step(n)

        groupeds = {}
        w_mx = {}

        items = [(n, 0, CHUNK) for n in range(PIECES - PASSES)]
        for half in range(2):
            items += [(n, CHUNK // 2 * half, CHUNK // 2 * (half + 1)) for n in range(PIECES - PASSES, PIECES)]

        def regroup_item(s):
            n, lo, hi = items[s]
            grouped = w_stage.tile([P, hi - lo, PACK], BF16, align_bytes=64, name="w_grouped")
            src = raws[n][:, :, lo:hi].rearrange("p j (c i) -> p c j i", i=RUN)
            dst = grouped[:].rearrange("p (c i) j -> p c j i", i=RUN)
            split = (VECTOR_COLS[n // CHUNK_PIECES][n % 2] if hi - lo == CHUNK else 0) // RUN
            nc.scalar.copy(out=dst[:, split:], in_=src[:, split:])
            if split:
                nc.vector.tensor_copy(out=dst[:, :split], in_=src[:, :split])
            groupeds[s] = grouped

        def quantise_item(s):
            n, lo, hi = items[s]
            g = n % PASSES
            if g == 0 and lo == 0:
                codes = w_pool.tile([P, PASSES, CHUNK], U32, align_bytes=64, name="w_codes")
                scales = w_pool.tile([P, PASSES, CHUNK], U8, align_bytes=64, name="w_scales")
                w_mx[n // PASSES] = (codes, scales)
            codes, scales = w_mx[n // PASSES]
            nc.vector.quantize_mx(
                out=codes[:, g, lo:hi].bitcast(FP8X4),
                scales=scales[:, g, lo:hi],
                in_=groupeds.pop(s)[:].rearrange("p c j -> p (c j)"),
            )

        units = [(m, pair, g) for m in range(2) for pair in range(TOKEN_TILES // 2) for g in range(PASSES)]
        flips = {}
        x_grouped = {}

        def flip_unit(k):
            m, pair, g = units[k]
            rows = (h_rows, c_rows)[m]
            flipped = psum_t.tile([P, 2, 2 * P], F32, name="t")
            for u in range(2):
                for s in range(2):
                    words = rows[:, 2 * pair + s, :].bitcast(F32)
                    nc.tensor.transpose(
                        flipped[:, u, P * s : P * (s + 1)],
                        words[:, 2 * P * g + P * u : 2 * P * g + P * (u + 1)],
                        ident_f32[:],
                    )
            flips[k] = flipped

        def group_unit(k):
            flipped = flips.pop(k)
            grouped = stage.tile([P, 2 * P * PACK], BF16, align_bytes=64, name="x_grouped")
            side_by_side = grouped[:].bitcast(F32).rearrange("p (r u) -> p r u", u=2)
            if k % 2 == 0:
                nc.vector.tensor_copy(out=side_by_side, in_=flipped[:].rearrange("p u r -> p r u"))
            else:
                nc.scalar.copy(out=side_by_side, in_=flipped[:].rearrange("p u r -> p r u"))
            x_grouped[k] = grouped

        def quantise_unit(k):
            m, pair, g = units[k]
            codes, scales = ((h_codes, h_scales), (c_codes, c_scales))[m]
            tokens = slice(2 * P * pair, 2 * P * (pair + 1))
            nc.vector.quantize_mx(
                out=codes[:, g, tokens].bitcast(FP8X4), scales=scales[:, g, tokens], in_=x_grouped.pop(k)[:]
            )

        gates = {}
        accs = {}

        def one_pass(acc, w, f, x_mx, g):
            features = slice(P * f, P * (f + 1))
            nc.tensor.matmul_mx(
                out=acc[:],
                lhsT=w[0][:, g, features].bitcast(FP8X4),
                lhsT_scale=w[1][:, g, features],
                rhs=x_mx[0][:, g, :].bitcast(FP8X4),
                rhs_scale=x_mx[1][:, g, :],
                start=(g == 0),
                stop=(g == PASSES - 1),
            )

        def product(which, chunk, f):
            acc = psum_acc.tile([P, TOKENS], F32, name="acc")
            x_mx = ((h_codes, h_scales), (c_codes, c_scales))[which]
            for g in range(PASSES):
                one_pass(acc, w_mx[2 * chunk + which], f, x_mx, g)
            accs[which, chunk, f] = acc

        def product_pass(which, chunk, g, features):
            x_mx = ((h_codes, h_scales), (c_codes, c_scales))[which]
            for f in features:
                if g == 0:
                    accs[which, chunk, f] = psum_acc.tile([P, TOKENS], F32, name="acc")
                one_pass(accs[which, chunk, f], w_mx[2 * chunk + which], f, x_mx, g)

        def sigmoid(chunk, f):
            if f == 0:
                gates[chunk] = work.tile([P, FEATURE_TILES, TOKENS], F32, name="gate")
            bg_col = n_tiles + FEATURE_TILES * chunk + f
            nc.scalar.activation(
                out=gates[chunk][:, f, :],
                in_=accs.pop((0, chunk, f))[:],
                func=ACT.Sigmoid,
                bias=bias_cols[:, bg_col : bg_col + 1],
                scale=1.0,
            )

        def apply_gate(chunk, f, tokens=slice(0, TOKENS)):
            bo_col = FEATURE_TILES * chunk + f
            gate = gates[chunk]
            nc.vector.scalar_tensor_tensor(
                out=gate[:, f, tokens],
                in0=accs[1, chunk, f][:, tokens],
                scalar=bias_cols[:, bo_col : bo_col + 1],
                in1=gate[:, f, tokens],
                op0=ALU.add,
                op1=ALU.mult,
            )

        backs = {}
        ALL, LOW, HIGH = range(FEATURE_TILES), range(FEATURE_TILES // 2), range(FEATURE_TILES // 2, FEATURE_TILES)

        def columns(chunk, features):
            return slice(CHUNK * chunk + P * features[0], CHUNK * chunk + P * (features[-1] + 1))

        def back_to_tokens(chunk, features, i):
            if features[0] == 0:
                backs[chunk, i] = psum_t.tile([P, CHUNK], F32, name="t")
            back = backs[chunk, i]
            nc.tensor.matmul(
                back[:, P * features[0] : P * (features[-1] + 1)],
                lhsT=ident_bf16[:],
                rhs=h_rows[:, i, columns(chunk, features)],
                start=True,
                stop=False,
            )
            for f in features:
                nc.tensor.matmul(
                    back[:, P * f : P * (f + 1)],
                    lhsT=gates[chunk][:, f, P * i : P * (i + 1)],
                    rhs=ident_f32[:],
                    is_transpose=True,
                    start=False,
                    stop=(f == features[-1]),
                )

        def take_stats(chunk, features, i):
            nc.vector.bn_stats(
                out=stats[:, i, chunk + (features[0] > 0), :],
                in_=backs[chunk, i][:, P * features[0] : P * (features[-1] + 1)],
            )

        def take_y(chunk, i):
            cols = columns(chunk, ALL)
            nc.vector.tensor_tensor(
                out=y_gamma[:, i, cols], in0=backs.pop((chunk, i))[:], in1=gamma_all[:, cols], op=ALU.mult
            )

        last = CHUNKS - 1
        due_s = {}
        due_v = {}
        due_pe = {}
        unit_jobs = {}
        for pair in range(TOKEN_TILES):
            unit_jobs[ACT_AFTER[2 * pair + 1] + 1] = unit_jobs.get(ACT_AFTER[2 * pair + 1] + 1, []) + list(range(PASSES * pair, PASSES * (pair + 1)))
        products = []
        for chunk in range(CHUNKS):
            for which in range(2):
                final = (which, chunk) == (1, last)
                features = LOW if final else ALL
                for f in features:
                    first = CHUNK_PIECES * chunk + PASSES * (which + 1) - 1 + (1 if final else LAG)
                    if chunk > 0 or which == 1:
                        products.append((which, chunk, features, f, max(first, ACT_AFTER[TOKEN_TILES * (which + 1) - 1] + 1)))
        for s in range(len(items) + 1):
            if s == BIAS_STEP:
                make_bias_cols()
                nc.sync.dma_start(out=norm_rows[0:1, :], in_=ln_gamma.unsqueeze(0))
                nc.sync.dma_start(out=norm_rows[1:2, :], in_=ln_gamma.unsqueeze(0))
                nc.sync.dma_start(out=norm_rows[2:3, :], in_=ln_beta.unsqueeze(0))
            if s == 9:
                nc.sync.dma_start(out=gamma_all[:], in_=ln_gamma.partition_broadcast(P))
            for job in due_s.pop(s, ()):
                job()
            now = unit_jobs.get(s, [])
            for i in range(0, len(now), 2):
                flip_unit(now[i])
                flip_unit(now[i + 1])
                group_unit(now[i])
                group_unit(now[i + 1])
                if i:
                    quantise_unit(now[i - 2])
                    quantise_unit(now[i - 1])
            if s < len(items):
                regroup_item(s)
            for k in now[-2:]:
                quantise_unit(k)
            load_step(s + AHEAD)
            if s >= 1:
                quantise_item(s - 1)
            for job in due_v.pop(s, ()):
                job()
            start = ACT_AFTER[TOKEN_TILES - 1] + 1
            if s == start:
                for g in range(s):
                    if g < PASSES:
                        product_pass(0, 0, g, ALL)
            elif start < s <= PASSES:
                product_pass(0, 0, s - 1, ALL)
            if s == max(start, PASSES):
                for f in ALL:
                    due_s.setdefault(s + 1, []).append(partial(sigmoid, 0, f))
            g = s - 1 - (len(items) - PASSES)
            if g >= 0:
                product_pass(1, last, g, HIGH)
            for turn in range(2 if s > PIECES - PASSES else GROUPS_PER_STEP):
                if products and products[0][4] <= s:
                    which, chunk, features, f, first = products.pop(0)
                    product(which, chunk, f)
                    if which == 0:
                        due_s.setdefault(s + 1, []).append(partial(sigmoid, chunk, f))
                    else:
                        due_v.setdefault(s + 1, []).append(partial(apply_gate, chunk, f))
                        if f == features[-1]:
                            for i in range(TOKEN_TILES):
                                t = s + (1 if features is LOW else 2) + i // BACKS
                                due_pe.setdefault(t, []).append(partial(back_to_tokens, chunk, features, i))
                                if features is LOW:
                                    due_v.setdefault(t + LOW_LAG, []).append(partial(take_stats, chunk, features, i))
                                else:
                                    due_v.setdefault(t + 1, []).append(partial(take_stats, chunk, features, i))
                                    due_v.setdefault(t + 1, []).append(partial(take_y, chunk, i))
            for job in due_pe.pop(s, ()):
                job()
        for due in (due_s, due_pe, due_v):
            for s in sorted(due):
                for job in due[s]:
                    job()
        assert not products

        rstd = keep.tile([P, TOKEN_TILES], F32)
        nc.scalar.activation(
            out=rstd[:, 0:1], in_=gates[last][:, 3, 0:1], func=ACT.Abs_reciprocal_sqrt, bias=eps_col[:], scale=1.0
        )
        pairs = [(0, 1), (2, 3)]
        for pair in pairs:
            for f in HIGH:
                apply_gate(last, f, slice(P * pair[0], P * (pair[-1] + 1)))
        for i in range(TOKEN_TILES):
            back_to_tokens(last, HIGH, i)

        mean_var = keep.tile([P, TOKEN_TILES, 2], F32)
        shift = keep.tile([P, TOKEN_TILES], F32)
        shift_rows = keep.tile([P, TOKENS], BF16)

        def aggregate(pair):
            for i in pair:
                take_stats(last, HIGH, i)
            for i in pair:
                nc.vector.bn_aggr(out=mean_var[:, i, :], in_=stats[:, i, :, :].rearrange("p c s -> p (c s)"))
            both = slice(pair[0], pair[-1] + 1)
            nc.scalar.activation(
                out=rstd[:, both], in_=mean_var[:, both, 1], func=ACT.Abs_reciprocal_sqrt, bias=eps_col[:], scale=1.0
            )

        def split_shift(pair):
            both = slice(pair[0], pair[-1] + 1)
            for out_ap in (shift_cols[:, both, 0], shift[:, both]):
                nc.vector.scalar_tensor_tensor(
                    out=out_ap, in0=mean_var[:, both, 0], scalar=-1.0, in1=rstd[:, both], op0=ALU.mult, op1=ALU.mult
                )

        def split_shift_low(pair):
            both = slice(pair[0], pair[-1] + 1)
            nc.vector.tensor_tensor(
                out=shift_cols[:, both, 1], in0=shift[:, both], in1=shift_cols[:, both, 0], op=ALU.subtract
            )

        def shift_to_rows(pair):
            flat = psum_acc.tile([P, 2 * P], BF16, name="acc")
            for i in pair:
                nc.tensor.transpose(flat[:, P * (i - pair[0]) : P * (i - pair[0] + 1)], shift_cols[:, i, :], ident_bf16[:])
            nc.scalar.copy(out=shift_rows[:, P * pair[0] : P * (pair[-1] + 1)], in_=flat[:])

        aggregate(pairs[0])
        take_y(last, 0)
        split_shift(pairs[0])
        aggregate(pairs[1])
        split_shift_low(pairs[0])
        shift_to_rows(pairs[0])
        take_y(last, 1)
        split_shift(pairs[1])
        split_shift_low(pairs[1])

        out_rows = out.rearrange("b s d -> s b d")
        for i in range(TOKEN_TILES):
            if i == 1:
                shift_to_rows(pairs[1])
            if i in pairs[1]:
                take_y(last, i)
            for c in range(CHUNKS):
                cols = slice(CHUNK * c, CHUNK * (c + 1))
                offset = psum_acc.tile([P, CHUNK], F32, name="acc")
                nc.tensor.matmul(
                    offset[:], lhsT=shift_rows[:, P * i : P * (i + 1)], rhs=norm_rows[:, cols], start=True, stop=True
                )
                nc.vector.scalar_tensor_tensor(
                    out=y_gamma[:, i, cols],
                    in0=y_gamma[:, i, cols],
                    scalar=rstd[:, i : i + 1],
                    in1=offset[:],
                    op0=ALU.mult,
                    op1=ALU.add,
                )
                if (i == 0 and c < CHUNKS // 2) or (i == TOKEN_TILES - 1 and c >= CHUNKS // 2):
                    nc.sync.dma_start(out=out_rows[:, i, cols], in_=y_gamma[:, i, cols])
                elif (c + 1) * CHUNK % LN_COLS == 0:
                    cols = slice((c + 1) * CHUNK - LN_COLS, (c + 1) * CHUNK)
                    nc.sync.dma_start(out=out_rows[:, i, cols], in_=y_gamma[:, i, cols])
